import numpy as np
import ml_dtypes


def mxq(x, axis, fmt="e4m3"):
    dtype, down = {"e4m3": (ml_dtypes.float8_e4m3fn, 7), "e5m2": (ml_dtypes.float8_e5m2, 14)}[fmt]
    v = np.moveaxis(np.asarray(x, np.float32).astype(ml_dtypes.bfloat16).astype(np.float64), axis, -1)
    blocks = v.reshape(v.shape[:-1] + (-1, 32))
    amax = np.abs(blocks).max(-1, keepdims=True)
    byte = np.maximum(np.where(amax > 0, np.frexp(amax)[1] - 1 + 127, 0) - down, 1)
    scale = np.exp2(byte - 127.0)
    codes = (blocks / scale).astype(np.float32).astype(dtype).astype(np.float64)
    return np.moveaxis((codes * scale).reshape(v.shape), -1, axis)


WIDE = False


def mx_kscale(k):
    if not WIDE:
        return np.ones(k)
    levels = np.array([10, -10, 5, -5, 0])
    a = np.random.permutation(np.resize(levels, k // 512 * 4)).reshape(k // 512, 4)
    idx = np.arange(k)
    return np.exp2(a[idx // 512, idx % 128 // 32])


BF16 = ml_dtypes.bfloat16


def bf(x):
    return np.asarray(x, np.float32).astype(BF16)


def f64(x):
    return np.asarray(x).astype(np.float64)


B, S, H = 4, 1024, 512
GAMMA = 0.96875


def sigmoid(v):
    return 1.0 / (1.0 + np.exp(-v))


def setup_inputs():
    s, u = mx_kscale(H), mx_kscale(H)
    a = 1.4 / H ** 0.25
    return {"q": bf(np.random.standard_normal((B, S, H)) * a * s),
            "k": bf(np.random.standard_normal((B, S, H)) * a / s),
            "x": bf(np.random.standard_normal((B, S, H)) * u),
            "w_v": bf(np.random.standard_normal((H, H)) * 0.5 / np.sqrt(H) / u[:, None])}


def reference(q, k, x, w_v):
    idx = f64(np.arange(S))
    decay = GAMMA ** np.abs(idx[None, :] - idx[:, None])
    scores = (mxq(f64(q), 2, "e4m3") @ mxq(f64(k), 2, "e4m3").transpose(0, 2, 1)) * decay
    g = scores * sigmoid(scores)
    v = mxq(f64(x), 2, "e4m3") @ mxq(f64(w_v), 0, "e4m3")
    return mxq(g, 2, "e4m3") @ mxq(v, 1, "e4m3")

@@ -1,0 +1,348 @@
+from contextlib import ExitStack
+
+import concourse.mybir as mybir
+from concourse.masks import make_identity
+
+F32 = mybir.dt.float32
+BF16 = mybir.dt.bfloat16
+U32 = mybir.dt.uint32
+U8 = mybir.dt.uint8
+FP8X4 = mybir.dt.float8_e4m3fn_x4
+ALU = mybir.AluOpType
+ACT = mybir.ActivationFunctionType
+
+B, S, H = 4, 1024, 512
+P = 128
+GAMMA = 0.96875
+FLOPS = 2 * B * S * H * H + 4 * B * S * S * H
+
+NSTEP = 64
+NFX = 5
+NSC = 3
+TW = 516
+PIN = True
+GATE_STEP, GATE_BASE = 1.25, 4.0
+V_SIDE = (1, 3, 5, 7)
+S_TWICE = (3, 7)
+FINE_FROM = 60
+
+
+def tile_simpleretention_pa_t_kernel(tc, q, k, x, w_v, out):
+    nc = tc.nc
+    src = {"q": q, "k": k, "x": x}
+    with ExitStack() as ctx:
+        const = ctx.enter_context(tc.tile_pool(name="const", bufs=1))
+        inp = ctx.enter_context(tc.tile_pool(name="inp", bufs=6))
+        work = ctx.enter_context(tc.tile_pool(name="work", bufs=2))
+        psum = ctx.enter_context(tc.psum_pool(name="psum", bufs=1))
+        if PIN:
+            ctx.enter_context(tc.manual_schedule())
+
+        raw = {}
+        place = {}
+
+        def load(name, b, g):
+            place[(name, b, g)] = len(place) + (1 if len(place) >= 4 else 0)
+            t = inp.tile([P, 2048], BF16, name="in_" + name, tag="in_" + name, bufs=6)
+            view = src[name][b].rearrange("(g p t) h -> g p (t h)", g=2, p=P, t=4)
+            nc.sync.dma_start(out=t[:], in_=view[g])
+            raw[(name, b, g)] = t
+
+        w_raw = const.tile([P, 2048], BF16, name="w_raw")
+        for b in range(B):
+            for name, g in (("k", 0), ("q", 0), ("k", 1), ("q", 1)):
+                load(name, b, g)
+            if b == 0:
+                nc.sync.dma_start(
+                    out=w_raw[:].rearrange("p (u f) -> p u f", u=2),
+                    in_=w_v.rearrange("(u p e) c -> p u (e c)", u=2, p=P, e=2),
+                )
+            load("x", b, 0)
+            load("x", b, 1)
+
+        ident = const.tile([P, P], F32, name="ident")
+        make_identity(nc, ident[:])
+
+        up = const.tile([P, TW], F32, name="up")
+        dn = const.tile([P, TW], F32, name="dn")
+        nc.vector.memset(up[:, 0:1], 1.0)
+        nc.vector.memset(dn[:, TW - 1 : TW], 1.0)
+        n = 1
+        while n < TW:
+            m = min(n, TW - n)
+            nc.vector.tensor_scalar_mul(out=up[:, n : n + m], in0=up[:, 0:m], scalar1=GAMMA**n)
+            nc.vector.tensor_scalar_mul(
+                out=dn[:, TW - n - m : TW - n], in0=dn[:, TW - m : TW], scalar1=GAMMA**n
+            )
+            n *= 2
+        rows = const.tile([P, 2 * P], F32, name="rows")
+        nc.vector.tensor_copy(out=rows[:, 0:P], in_=up[:, 0:512].rearrange("p (a f) -> p a f", f=4)[:, :, 0])
+        nc.vector.tensor_copy(out=rows[:, P : 2 * P], in_=dn[:, 4:516].rearrange("p (a f) -> p a f", f=4)[:, :, 3])
+        cols_ps = psum.tile([P, 512], F32, name="fx", tag="fx", bufs=NFX)
+        nc.tensor.transpose(out=cols_ps[:, 0:P], in_=rows[:, 0:P], identity=ident[:])
+        nc.tensor.transpose(out=cols_ps[:, P : 2 * P], in_=rows[:, P : 2 * P], identity=ident[:])
+        cols = const.tile([P, 2], F32, name="cols")
+        nc.vector.tensor_copy(out=cols[:], in_=cols_ps[:, 0 : 2 * P].rearrange("p (a c) -> p a c", a=2)[:, :, 0])
+        ZW = 515
+        z_hi = const.tile([P, TW], F32, name="z_hi")
+        z_lo = const.tile([P, TW], F32, name="z_lo")
+        z_eq = const.tile([P, TW], F32, name="z_eq")
+        nc.vector.tensor_scalar_mul(out=z_hi[:, 0:ZW], in0=dn[:, 0:ZW], scalar1=cols[:, 0:1])
+        nc.vector.tensor_scalar_mul(out=z_lo[:, 0:ZW], in0=up[:, 1 : ZW + 1], scalar1=cols[:, 1:2])
+        nc.vector.tensor_tensor(out=z_eq[:, 0:ZW], in0=z_hi[:, 0:ZW], in1=z_lo[:, 0:ZW], op=ALU.min)
+        nc.vector.tensor_scalar_mul(out=z_eq[:, 0:ZW], in0=z_eq[:, 0:ZW], scalar1=GAMMA ** (-512))
+        decay = {1: z_hi, -1: z_lo, 0: z_eq}
+
+        grp = {}
+        codes = {}
+        outs = []
+        have = set()
+        NBUF = {"k": 4, "q": 4, "x": 3, "v": 6, "g": 6, "w": 1}
+
+        def drain(eng, out_ap, in_ap):
+            if eng == "S":
+                nc.scalar.copy(out=out_ap, in_=in_ap)
+            else:
+                nc.vector.tensor_copy(out=out_ap, in_=in_ap)
+
+        def new_grp(key):
+            if key[0] == "w":
+                grp[key] = const.tile([P, 2048], BF16, name="w_grp", align_bytes=64)
+            elif key[0] == "g":
+                grp[key] = work.tile([P, 2048], BF16, name="swi", tag="swi", bufs=3, align_bytes=64)
+            else:
+                grp[key] = work.tile([P, 2048], BF16, name="grp", tag="grp", bufs=4, align_bytes=64)
+
+        def quantise(key):
+            kind = key[0]
+            c = work.tile([P, 512], U32, name="c_" + kind, tag="c_" + kind, bufs=NBUF[kind], align_bytes=64)
+            s = work.tile([P, 512], U8, name="s_" + kind, tag="s_" + kind, bufs=NBUF[kind], align_bytes=64)
+            nc.vector.quantize_mx(out=c[:].bitcast(FP8X4), scales=s[:], in_=grp[key][:])
+            codes[key] = (c, s)
+            have.add(key)
+            if kind == "g" and key[3] == 1:
+                for tq in range(4):
+                    outs.append((key[1], key[2], tq))
+
+        def quantise_block(arg):
+            key, tq = arg
+            if tq == 0:
+                c = work.tile([P, 512], U32, name="c_g", tag="c_g", bufs=NBUF["g"], align_bytes=64)
+                s = work.tile([P, 512], U8, name="s_g", tag="s_g", bufs=NBUF["g"], align_bytes=64)
+                codes[key] = (c, s)
+            c, s = codes[key]
+            nc.vector.quantize_mx(
+                out=c[:, tq * P : (tq + 1) * P].bitcast(FP8X4),
+                scales=s[:, tq * P : (tq + 1) * P],
+                in_=grp[key][:, tq * 512 : (tq + 1) * 512],
+            )
+            if key[3] == 1:
+                outs.append((key[1], key[2], tq))
+
+        def mx(out_ap, lhs, lcol, rhs, rcol, width, start=True, stop=True):
+            nc.tensor.matmul_mx(
+                out=out_ap,
+                lhsT=lhs[0][:, lcol : lcol + P].bitcast(FP8X4),
+                lhsT_scale=lhs[1][:, lcol : lcol + P],
+                rhs=rhs[0][:, rcol : rcol + width].bitcast(FP8X4),
+                rhs_scale=rhs[1][:, rcol : rcol + width],
+                start=start,
+                stop=stop,
+            )
+
+        def fx_bank():
+            return psum.tile([P, 512], F32, name="fx", tag="fx", bufs=NFX)
+
+        def pe_transposes(name, b, g):
+            words = raw[(name, b, g)][:].bitcast(F32)
+            res = []
+            for a in range(2):
+                bank = fx_bank()
+                for c in range(4):
+                    col = (2 * a + c // 2) * 256 + (c % 2) * P
+                    nc.tensor.transpose(out=bank[:, c * P : (c + 1) * P], in_=words[:, col : col + P], identity=ident[:])
+                res.append(("T", (name, b, g), a, bank))
+            return res
+
+        def exit_transposes(eng, key, a, bank):
+            if a == 0:
+                new_grp(key)
+            dst = grp[key][:].bitcast(F32)[:, a * 512 : (a + 1) * 512]
+            drain(
+                eng,
+                dst.rearrange("p (a r u) -> p a r u", a=2, u=2),
+                bank[:].rearrange("p (a u r) -> p a r u", a=2, u=2),
+            )
+
+        def pe_v(b, g, hb):
+            bank = fx_bank()
+            for s4 in range(4):
+                mx(bank[:, s4 * P : (s4 + 1) * P], codes[("x", b, g)], (3 - s4) * P, codes[("w",)], hb * P, P)
+            return [("V", ("v", b, g), hb, bank)]
+
+        def exit_v(eng, key, hb, bank):
+            if hb == 0:
+                new_grp(key)
+            drain(
+                eng,
+                grp[key][:, hb * 512 : (hb + 1) * 512].rearrange("p (w s) -> p w s", s=4),
+                bank[:].rearrange("p (s w) -> p w s", s=4),
+            )
+
+        def step_ids(i):
+            return i // 16, (i % 16) // 8, (i % 8) // 4, i % 4
+
+        sc_bank = {}
+        tmp = {}
+
+        def pe_scores(i):
+            b, gq, gk, tq = step_ids(i)
+            bank = psum.tile([P, 512], F32, name="sc", tag="sc", bufs=NSC)
+            for s4 in range(4):
+                mx(bank[:, s4 * P : (s4 + 1) * P], codes[("k", b, gk)], (3 - s4) * P, codes[("q", b, gq)], tq * P, P)
+            sc_bank[i] = bank
+
+        def v_decay(i):
+            b, gq, gk, tq = step_ids(i)
+            t = work.tile([P, 512], F32, name="tmp", tag="tmp", bufs=4)
+            nc.vector.tensor_tensor(
+                out=t[:].rearrange("p (j s) -> p j s", s=4),
+                in0=sc_bank[i][:].rearrange("p (s j) -> p j s", s=4),
+                in1=decay[gk - gq][:, tq : tq + 512].rearrange("p (j s) -> p j s", s=4),
+                op=ALU.mult,
+            )
+            tmp[i] = t
+
+        def s_swish(i):
+            b, gq, gk, tq = step_ids(i)
+            key = ("g", b, gq, gk)
+            if tq == 0:
+                new_grp(key)
+            nc.scalar.activation(out=grp[key][:, tq * 512 : (tq + 1) * 512], in_=tmp[i][:], func=ACT.Silu)
+
+        def pe_out(b, gq, tq):
+            bank = fx_bank()
+            for gk in range(2):
+                mx(bank[:], codes[("g", b, gq, gk)], tq * P, codes[("v", b, gk)], 0, 512, start=(gk == 0), stop=(gk == 1))
+            return [("O", (b, gq), tq, bank)]
+
+        stage = {}
+
+        def exit_out(eng, key, tq, bank):
+            if tq == 0:
+                stage[key] = work.tile([P, 2048], F32, name="ost", tag="ost", bufs=3)
+            drain(eng, stage[key][:, tq * 512 : (tq + 1) * 512], bank[:])
+            b, gq = key
+            if (b, gq) == (B - 1, 1):
+                view = out[b].rearrange("(g j t) h -> g t j h", g=2, j=P, t=4)
+                nc.sync.dma_start(out=view[gq, tq], in_=stage[key][:, tq * 512 : (tq + 1) * 512])
+            elif tq == 3:
+                view = out[b].rearrange("(g j t) h -> g j (t h)", g=2, j=P, t=4)
+                nc.sync.dma_start(out=view[gq], in_=stage[key][:])
+
+        prep = []
+        for b in range(B):
+            for name, g in (("k", 0), ("q", 0), ("k", 1), ("q", 1), ("x", 0), ("x", 1)):
+                prep.append(("T", name, b, g))
+            for g in range(2):
+                for hb in range(4):
+                    prep.append(("V", b, g, hb))
+        pending = []
+        state = {"prep": 0, "sc": 0, "outs": 0, "pending": 0, "due": []}
+
+        def w_regroup(arg):
+            new_grp(("w",))
+            nc.vector.tensor_copy(
+                out=grp[("w",)][:].rearrange("p (c t) -> p c t", t=4),
+                in_=w_raw[:].rearrange("p (t c) -> p c t", t=4),
+            )
+
+        state["due"].append((0, w_regroup, None))
+        state["due"].append((1, quantise, ("w",)))
+
+        def next_side(slot):
+            room = NFX - (len(pending) - state["pending"])
+            if state["outs"] < len(outs) and room >= 1:
+                b, gq, tq = outs[state["outs"]]
+                if ("v", b, 0) in have and ("v", b, 1) in have:
+                    state["outs"] += 1
+                    return pe_out(b, gq, tq)
+            if state["prep"] < len(prep):
+                job = prep[state["prep"]]
+                if (
+                    job[0] == "T"
+                    and room >= 2
+                    and slot >= 16 * (job[2] - 1) - 8
+                    and slot >= GATE_STEP * place[(job[1], job[2], job[3])] - GATE_BASE
+                ):
+                    state["prep"] += 1
+                    return pe_transposes(job[1], job[2], job[3])
+                if job[0] == "V" and room >= 1 and ("x", job[1], job[2]) in have and ("w",) in have:
+                    state["prep"] += 1
+                    return pe_v(job[1], job[2], job[3])
+            return None
+
+        def side_exit(eng, slot):
+            if state["pending"] == len(pending):
+                return
+            kind, key, part, bank = pending[state["pending"]]
+            state["pending"] += 1
+            if kind == "T":
+                exit_transposes(eng, key, part, bank)
+                if part == 1:
+                    state["due"].append((slot + 1, quantise, key))
+            elif kind == "V":
+                exit_v(eng, key, part, bank)
+                if part == 3:
+                    state["due"].append((slot + 1, quantise, key))
+            else:
+                exit_out(eng, key, part, bank)
+
+        def vector_due(slot):
+            now = [item for item in state["due"] if item[0] <= slot]
+            state["due"] = [item for item in state["due"] if item[0] > slot]
+            for item in now:
+                item[1](item[2])
+
+        def swish_of(i, slot):
+            s_swish(i)
+            b, gq, gk, tq = step_ids(i)
+            if i >= FINE_FROM:
+                state["due"].append((slot + 1, quantise_block, (("g", b, gq, gk), tq)))
+            elif tq == 3:
+                state["due"].append((slot + 1, quantise, ("g", b, gq, gk)))
+
+        slot = -2
+        while True:
+            while state["sc"] < NSTEP and state["sc"] <= slot + 2:
+                b, gq, gk, tq = step_ids(state["sc"])
+                if ("k", b, gk) not in have or ("q", b, gq) not in have:
+                    break
+                pe_scores(state["sc"])
+                state["sc"] += 1
+            while True:
+                got = next_side(slot)
+                if got is None:
+                    break
+                pending.extend(got)
+            if 0 <= slot < NSTEP:
+                assert state["sc"] > slot, "scores of step %d are late" % slot
+                if slot >= 1:
+                    swish_of(slot - 1, slot)
+                side_exit("S", slot)
+                if slot % 8 in S_TWICE:
+                    side_exit("S", slot)
+                v_decay(slot)
+                if slot % 8 in V_SIDE:
+                    side_exit("V", slot)
+                vector_due(slot)
+            else:
+                vector_due(slot)
+                if slot == NSTEP:
+                    swish_of(slot - 1, slot)
+                for eng in ("S", "V", "S", "V"):
+                    side_exit(eng, slot)
+            slot += 1
+            idle = state["pending"] == len(pending) and not state["due"] and state["outs"] == len(outs)
+            if slot > NSTEP and idle and state["prep"] == len(prep):
+                break

@@ -22,8 +22,8 @@ NSC = 3
 TW = 516
 PIN = True
 GATE_STEP, GATE_BASE = 1.25, 4.0
-V_SIDE = (1, 3, 5, 7)
-S_TWICE = (3, 7)
+V_SIDE = (3, 7)
+S_TWICE = (1, 3, 5, 7)
 FINE_FROM = 60
 
 

@@ -20,10 +20,10 @@ NSTEP = 64
 NFX = 5
 NSC = 3
 TW = 516
-PIN = True
+PIN = False
 GATE_STEP, GATE_BASE = 1.25, 4.0
-V_SIDE = (3, 7)
-S_TWICE = (1, 3, 5, 7)
+V_SIDE = (1, 3, 5, 7)
+S_TWICE = (3, 7)
 FINE_FROM = 60
 
 

@@ -12,49 +12,70 @@ ALU = mybir.AluOpType
 ACT = mybir.ActivationFunctionType
 
 B, S, H = 4, 1024, 512
-P = 128
 GAMMA = 0.96875
 FLOPS = 2 * B * S * H * H + 4 * B * S * S * H
 
-NSTEP = 64
-NFX = 5
-NSC = 3
-TW = 516
-PIN = False
-GATE_STEP, GATE_BASE = 1.25, 4.0
-V_SIDE = (1, 3, 5, 7)
-S_TWICE = (3, 7)
-FINE_FROM = 60
+P = 128
+PACK = 4
+PASS = P * PACK
+BANK = 512
+GROUP = PASS * PACK
+
+STEPS = B * 2 * 2 * PACK
+STEPS_PER_SEQ = STEPS // B
+SCORE_BANKS = 3
+SIDE_BANKS = 5
+SCORES_AHEAD = 2
+
+S_TWICE = (2, 5, 7)
+V_SIDE = (1, 4, 7)
+
+LOAD_PACE, LOAD_LEAD = 1.25, 4.0
+HALVED_LOADS = 2
+FIRST_SLOT = -2
+LAST_ROUND = STEPS - PACK
+
+TABLE = PASS + PACK
+WINDOWS = BANK + PACK - 1
+
+LOAD_BUFS = 6
+CODE_BUFS = {"k": 4, "q": 4, "x": 3, "v": 6, "g": 6, "w": 1}
+GROUPED_BUFS = 6
+SWISH_BUFS = 4
+DECAYED_BUFS = 6
+STAGED_BUFS = 3
 
 
 def tile_simpleretention_pa_t_kernel(tc, q, k, x, w_v, out):
     nc = tc.nc
-    src = {"q": q, "k": k, "x": x}
+    inputs = {"q": q, "k": k, "x": x}
     with ExitStack() as ctx:
         const = ctx.enter_context(tc.tile_pool(name="const", bufs=1))
-        inp = ctx.enter_context(tc.tile_pool(name="inp", bufs=6))
+        loads = ctx.enter_context(tc.tile_pool(name="loads", bufs=LOAD_BUFS))
         work = ctx.enter_context(tc.tile_pool(name="work", bufs=2))
         psum = ctx.enter_context(tc.psum_pool(name="psum", bufs=1))
-        if PIN:
-            ctx.enter_context(tc.manual_schedule())
 
-        raw = {}
+        loaded = {}
         place = {}
 
         def load(name, b, g):
             place[(name, b, g)] = len(place) + (1 if len(place) >= 4 else 0)
-            t = inp.tile([P, 2048], BF16, name="in_" + name, tag="in_" + name, bufs=6)
-            view = src[name][b].rearrange("(g p t) h -> g p (t h)", g=2, p=P, t=4)
-            nc.sync.dma_start(out=t[:], in_=view[g])
-            raw[(name, b, g)] = t
+            tile = loads.tile([P, GROUP], BF16, name="in_" + name, tag="in_" + name, bufs=LOAD_BUFS)
+            rows = inputs[name][b].rearrange("(g p t) h -> g p (t h)", g=2, p=P, t=PACK)[g]
+            if len(place) <= HALVED_LOADS:
+                nc.sync.dma_start(out=tile[:, 0 : GROUP // 2], in_=rows[:, 0 : GROUP // 2])
+                nc.sync.dma_start(out=tile[:, GROUP // 2 : GROUP], in_=rows[:, GROUP // 2 : GROUP])
+            else:
+                nc.sync.dma_start(out=tile[:], in_=rows)
+            loaded[(name, b, g)] = tile
 
-        w_raw = const.tile([P, 2048], BF16, name="w_raw")
+        w_rows = const.tile([P, GROUP], BF16, name="w_rows")
         for b in range(B):
             for name, g in (("k", 0), ("q", 0), ("k", 1), ("q", 1)):
                 load(name, b, g)
             if b == 0:
                 nc.sync.dma_start(
-                    out=w_raw[:].rearrange("p (u f) -> p u f", u=2),
+                    out=w_rows[:].rearrange("p (u f) -> p u f", u=2),
                     in_=w_v.rearrange("(u p e) c -> p u (e c)", u=2, p=P, e=2),
                 )
             load("x", b, 0)
@@ -63,286 +84,305 @@ def tile_simpleretention_pa_t_kernel(tc, q, k, x, w_v, out):
         ident = const.tile([P, P], F32, name="ident")
         make_identity(nc, ident[:])
 
-        up = const.tile([P, TW], F32, name="up")
-        dn = const.tile([P, TW], F32, name="dn")
-        nc.vector.memset(up[:, 0:1], 1.0)
-        nc.vector.memset(dn[:, TW - 1 : TW], 1.0)
-        n = 1
-        while n < TW:
-            m = min(n, TW - n)
-            nc.vector.tensor_scalar_mul(out=up[:, n : n + m], in0=up[:, 0:m], scalar1=GAMMA**n)
+        rising = const.tile([P, TABLE], F32, name="rising")
+        falling = const.tile([P, TABLE], F32, name="falling")
+        nc.vector.memset(rising[:, 0:1], 1.0)
+        nc.vector.memset(falling[:, TABLE - 1 : TABLE], 1.0)
+        done = 1
+        while done < TABLE:
+            more = min(done, TABLE - done)
+            nc.vector.tensor_scalar_mul(out=rising[:, done : done + more], in0=rising[:, 0:more], scalar1=GAMMA**done)
             nc.vector.tensor_scalar_mul(
-                out=dn[:, TW - n - m : TW - n], in0=dn[:, TW - m : TW], scalar1=GAMMA**n
+                out=falling[:, TABLE - done - more : TABLE - done],
+                in0=falling[:, TABLE - more : TABLE],
+                scalar1=GAMMA**done,
             )
-            n *= 2
-        rows = const.tile([P, 2 * P], F32, name="rows")
-        nc.vector.tensor_copy(out=rows[:, 0:P], in_=up[:, 0:512].rearrange("p (a f) -> p a f", f=4)[:, :, 0])
-        nc.vector.tensor_copy(out=rows[:, P : 2 * P], in_=dn[:, 4:516].rearrange("p (a f) -> p a f", f=4)[:, :, 3])
-        cols_ps = psum.tile([P, 512], F32, name="fx", tag="fx", bufs=NFX)
-        nc.tensor.transpose(out=cols_ps[:, 0:P], in_=rows[:, 0:P], identity=ident[:])
-        nc.tensor.transpose(out=cols_ps[:, P : 2 * P], in_=rows[:, P : 2 * P], identity=ident[:])
-        cols = const.tile([P, 2], F32, name="cols")
-        nc.vector.tensor_copy(out=cols[:], in_=cols_ps[:, 0 : 2 * P].rearrange("p (a c) -> p a c", a=2)[:, :, 0])
-        ZW = 515
-        z_hi = const.tile([P, TW], F32, name="z_hi")
-        z_lo = const.tile([P, TW], F32, name="z_lo")
-        z_eq = const.tile([P, TW], F32, name="z_eq")
-        nc.vector.tensor_scalar_mul(out=z_hi[:, 0:ZW], in0=dn[:, 0:ZW], scalar1=cols[:, 0:1])
-        nc.vector.tensor_scalar_mul(out=z_lo[:, 0:ZW], in0=up[:, 1 : ZW + 1], scalar1=cols[:, 1:2])
-        nc.vector.tensor_tensor(out=z_eq[:, 0:ZW], in0=z_hi[:, 0:ZW], in1=z_lo[:, 0:ZW], op=ALU.min)
-        nc.vector.tensor_scalar_mul(out=z_eq[:, 0:ZW], in0=z_eq[:, 0:ZW], scalar1=GAMMA ** (-512))
-        decay = {1: z_hi, -1: z_lo, 0: z_eq}
+            done *= 2
+        rows4 = const.tile([P, 2 * P], F32, name="rows4")
+        nc.vector.tensor_copy(
+            out=rows4[:, 0:P], in_=rising[:, 0:PASS].rearrange("p (a f) -> p a f", f=PACK)[:, :, 0]
+        )
+        nc.vector.tensor_copy(
+            out=rows4[:, P : 2 * P], in_=falling[:, PACK:TABLE].rearrange("p (a f) -> p a f", f=PACK)[:, :, PACK - 1]
+        )
+        turned = psum.tile([P, BANK], F32, name="side", tag="side", bufs=SIDE_BANKS)
+        nc.tensor.transpose(out=turned[:, 0:P], in_=rows4[:, 0:P], identity=ident[:])
+        nc.tensor.transpose(out=turned[:, P : 2 * P], in_=rows4[:, P : 2 * P], identity=ident[:])
+        by_part = const.tile([P, 2], F32, name="by_part")
+        nc.vector.tensor_copy(out=by_part[:], in_=turned[:, 0 : 2 * P].rearrange("p (a c) -> p a c", a=2)[:, :, 0])
+        above = const.tile([P, TABLE], F32, name="above")
+        below = const.tile([P, TABLE], F32, name="below")
+        level = const.tile([P, TABLE], F32, name="level")
+        nc.vector.tensor_scalar_mul(out=above[:, 0:WINDOWS], in0=falling[:, 0:WINDOWS], scalar1=by_part[:, 0:1])
+        nc.vector.tensor_scalar_mul(out=below[:, 0:WINDOWS], in0=rising[:, 1 : WINDOWS + 1], scalar1=by_part[:, 1:2])
+        nc.vector.tensor_tensor(out=level[:, 0:WINDOWS], in0=above[:, 0:WINDOWS], in1=below[:, 0:WINDOWS], op=ALU.min)
+        nc.vector.tensor_scalar_mul(out=level[:, 0:WINDOWS], in0=level[:, 0:WINDOWS], scalar1=GAMMA ** (-PASS))
+        decay = {1: above, -1: below, 0: level}
 
-        grp = {}
+        grouped = {}
         codes = {}
-        outs = []
-        have = set()
-        NBUF = {"k": 4, "q": 4, "x": 3, "v": 6, "g": 6, "w": 1}
+        quantised = set()
+        out_ready = []
 
-        def drain(eng, out_ap, in_ap):
-            if eng == "S":
-                nc.scalar.copy(out=out_ap, in_=in_ap)
+        def empty_bank(engine, dst, src):
+            if engine == "scalar":
+                nc.scalar.copy(out=dst, in_=src)
             else:
-                nc.vector.tensor_copy(out=out_ap, in_=in_ap)
+                nc.vector.tensor_copy(out=dst, in_=src)
 
-        def new_grp(key):
+        def new_grouped(key):
             if key[0] == "w":
-                grp[key] = const.tile([P, 2048], BF16, name="w_grp", align_bytes=64)
+                grouped[key] = const.tile([P, GROUP], BF16, name="w_grouped", align_bytes=64)
             elif key[0] == "g":
-                grp[key] = work.tile([P, 2048], BF16, name="swi", tag="swi", bufs=3, align_bytes=64)
+                grouped[key] = work.tile([P, GROUP], BF16, name="swish", tag="swish", bufs=SWISH_BUFS, align_bytes=64)
             else:
-                grp[key] = work.tile([P, 2048], BF16, name="grp", tag="grp", bufs=4, align_bytes=64)
+                grouped[key] = work.tile([P, GROUP], BF16, name="grouped", tag="grouped", bufs=GROUPED_BUFS, align_bytes=64)
+
+        def new_codes(key):
+            kind = key[0]
+            words = work.tile(
+                [P, PASS], U32, name="words_" + kind, tag="words_" + kind, bufs=CODE_BUFS[kind], align_bytes=64
+            )
+            scales = work.tile(
+                [P, PASS], U8, name="scales_" + kind, tag="scales_" + kind, bufs=CODE_BUFS[kind], align_bytes=64
+            )
+            codes[key] = (words, scales)
 
         def quantise(key):
-            kind = key[0]
-            c = work.tile([P, 512], U32, name="c_" + kind, tag="c_" + kind, bufs=NBUF[kind], align_bytes=64)
-            s = work.tile([P, 512], U8, name="s_" + kind, tag="s_" + kind, bufs=NBUF[kind], align_bytes=64)
-            nc.vector.quantize_mx(out=c[:].bitcast(FP8X4), scales=s[:], in_=grp[key][:])
-            codes[key] = (c, s)
-            have.add(key)
-            if kind == "g" and key[3] == 1:
-                for tq in range(4):
-                    outs.append((key[1], key[2], tq))
+            new_codes(key)
+            words, scales = codes[key]
+            nc.vector.quantize_mx(out=words[:].bitcast(FP8X4), scales=scales[:], in_=grouped[key][:])
+            quantised.add(key)
+            if key[0] == "g" and key[3] == 1:
+                for tq in range(PACK):
+                    out_ready.append((key[1], key[2], tq))
 
-        def quantise_block(arg):
-            key, tq = arg
+        def quantise_query_block(key_and_block):
+            key, tq = key_and_block
             if tq == 0:
-                c = work.tile([P, 512], U32, name="c_g", tag="c_g", bufs=NBUF["g"], align_bytes=64)
-                s = work.tile([P, 512], U8, name="s_g", tag="s_g", bufs=NBUF["g"], align_bytes=64)
-                codes[key] = (c, s)
-            c, s = codes[key]
+                new_codes(key)
+            words, scales = codes[key]
             nc.vector.quantize_mx(
-                out=c[:, tq * P : (tq + 1) * P].bitcast(FP8X4),
-                scales=s[:, tq * P : (tq + 1) * P],
-                in_=grp[key][:, tq * 512 : (tq + 1) * 512],
+                out=words[:, tq * P : (tq + 1) * P].bitcast(FP8X4),
+                scales=scales[:, tq * P : (tq + 1) * P],
+                in_=grouped[key][:, tq * BANK : (tq + 1) * BANK],
             )
             if key[3] == 1:
-                outs.append((key[1], key[2], tq))
+                out_ready.append((key[1], key[2], tq))
 
-        def mx(out_ap, lhs, lcol, rhs, rcol, width, start=True, stop=True):
+        def matmul_mx(dst, stationary, first_m, moving, first_n, width, start=True, stop=True):
             nc.tensor.matmul_mx(
-                out=out_ap,
-                lhsT=lhs[0][:, lcol : lcol + P].bitcast(FP8X4),
-                lhsT_scale=lhs[1][:, lcol : lcol + P],
-                rhs=rhs[0][:, rcol : rcol + width].bitcast(FP8X4),
-                rhs_scale=rhs[1][:, rcol : rcol + width],
+                out=dst,
+                lhsT=stationary[0][:, first_m : first_m + P].bitcast(FP8X4),
+                lhsT_scale=stationary[1][:, first_m : first_m + P],
+                rhs=moving[0][:, first_n : first_n + width].bitcast(FP8X4),
+                rhs_scale=moving[1][:, first_n : first_n + width],
                 start=start,
                 stop=stop,
             )
 
-        def fx_bank():
-            return psum.tile([P, 512], F32, name="fx", tag="fx", bufs=NFX)
+        def four_row_tiles(bank, tokens, moving, first_n):
+            for s in range(PACK):
+                matmul_mx(bank[:, s * P : (s + 1) * P], tokens, (PACK - 1 - s) * P, moving, first_n, P)
 
-        def pe_transposes(name, b, g):
-            words = raw[(name, b, g)][:].bitcast(F32)
-            res = []
-            for a in range(2):
-                bank = fx_bank()
+        def side_bank():
+            return psum.tile([P, BANK], F32, name="side", tag="side", bufs=SIDE_BANKS)
+
+        def tensor_transposes(name, b, g):
+            words = loaded[(name, b, g)][:].bitcast(F32)
+            banks = []
+            for part in range(2):
+                bank = side_bank()
                 for c in range(4):
-                    col = (2 * a + c // 2) * 256 + (c % 2) * P
-                    nc.tensor.transpose(out=bank[:, c * P : (c + 1) * P], in_=words[:, col : col + P], identity=ident[:])
-                res.append(("T", (name, b, g), a, bank))
-            return res
+                    first = (2 * part + c // 2) * (H // 2) + (c % 2) * P
+                    nc.tensor.transpose(
+                        out=bank[:, c * P : (c + 1) * P], in_=words[:, first : first + P], identity=ident[:]
+                    )
+                banks.append(("transposes", (name, b, g), part, bank))
+            return banks
 
-        def exit_transposes(eng, key, a, bank):
-            if a == 0:
-                new_grp(key)
-            dst = grp[key][:].bitcast(F32)[:, a * 512 : (a + 1) * 512]
-            drain(
-                eng,
+        def empty_transposes(engine, key, part, bank):
+            if part == 0:
+                new_grouped(key)
+            dst = grouped[key][:].bitcast(F32)[:, part * BANK : (part + 1) * BANK]
+            empty_bank(
+                engine,
                 dst.rearrange("p (a r u) -> p a r u", a=2, u=2),
                 bank[:].rearrange("p (a u r) -> p a r u", a=2, u=2),
             )
 
-        def pe_v(b, g, hb):
-            bank = fx_bank()
-            for s4 in range(4):
-                mx(bank[:, s4 * P : (s4 + 1) * P], codes[("x", b, g)], (3 - s4) * P, codes[("w",)], hb * P, P)
-            return [("V", ("v", b, g), hb, bank)]
+        def tensor_v(b, g, part):
+            bank = side_bank()
+            four_row_tiles(bank, codes[("x", b, g)], codes[("w",)], part * P)
+            return [("v", ("v", b, g), part, bank)]
 
-        def exit_v(eng, key, hb, bank):
-            if hb == 0:
-                new_grp(key)
-            drain(
-                eng,
-                grp[key][:, hb * 512 : (hb + 1) * 512].rearrange("p (w s) -> p w s", s=4),
-                bank[:].rearrange("p (s w) -> p w s", s=4),
+        def empty_v(engine, key, part, bank):
+            if part == 0:
+                new_grouped(key)
+            empty_bank(
+                engine,
+                grouped[key][:, part * BANK : (part + 1) * BANK].rearrange("p (w s) -> p w s", s=PACK),
+                bank[:].rearrange("p (s w) -> p w s", s=PACK),
             )
+
+        def tensor_out(b, gq, tq):
+            bank = side_bank()
+            for gk in range(2):
+                matmul_mx(
+                    bank[:], codes[("g", b, gq, gk)], tq * P, codes[("v", b, gk)], 0, BANK, start=(gk == 0), stop=(gk == 1)
+                )
+            return [("out", (b, gq), tq, bank)]
+
+        staged = {}
+
+        def empty_out(engine, key, tq, bank):
+            if tq == 0:
+                staged[key] = work.tile([P, PACK * BANK], F32, name="staged", tag="staged", bufs=STAGED_BUFS)
+            empty_bank(engine, staged[key][:, tq * BANK : (tq + 1) * BANK], bank[:])
+            b, gq = key
+            if key == (B - 1, 1):
+                rows = out[b].rearrange("(g j t) h -> g t j h", g=2, j=P, t=PACK)
+                nc.sync.dma_start(out=rows[gq, tq], in_=staged[key][:, tq * BANK : (tq + 1) * BANK])
+            elif tq == PACK - 1:
+                rows = out[b].rearrange("(g j t) h -> g j (t h)", g=2, j=P, t=PACK)
+                nc.sync.dma_start(out=rows[gq], in_=staged[key][:])
 
         def step_ids(i):
-            return i // 16, (i % 16) // 8, (i % 8) // 4, i % 4
+            return i // STEPS_PER_SEQ, (i % STEPS_PER_SEQ) // 8, (i % 8) // PACK, i % PACK
 
-        sc_bank = {}
-        tmp = {}
+        score_bank = {}
+        decayed = {}
 
-        def pe_scores(i):
+        def tensor_scores(i):
             b, gq, gk, tq = step_ids(i)
-            bank = psum.tile([P, 512], F32, name="sc", tag="sc", bufs=NSC)
-            for s4 in range(4):
-                mx(bank[:, s4 * P : (s4 + 1) * P], codes[("k", b, gk)], (3 - s4) * P, codes[("q", b, gq)], tq * P, P)
-            sc_bank[i] = bank
+            bank = psum.tile([P, BANK], F32, name="scores", tag="scores", bufs=SCORE_BANKS)
+            four_row_tiles(bank, codes[("k", b, gk)], codes[("q", b, gq)], tq * P)
+            score_bank[i] = bank
 
-        def v_decay(i):
+        def vector_decay(i):
             b, gq, gk, tq = step_ids(i)
-            t = work.tile([P, 512], F32, name="tmp", tag="tmp", bufs=4)
+            product = work.tile([P, BANK], F32, name="decayed", tag="decayed", bufs=DECAYED_BUFS)
             nc.vector.tensor_tensor(
-                out=t[:].rearrange("p (j s) -> p j s", s=4),
-                in0=sc_bank[i][:].rearrange("p (s j) -> p j s", s=4),
-                in1=decay[gk - gq][:, tq : tq + 512].rearrange("p (j s) -> p j s", s=4),
+                out=product[:].rearrange("p (j s) -> p j s", s=PACK),
+                in0=score_bank[i][:].rearrange("p (s j) -> p j s", s=PACK),
+                in1=decay[gk - gq][:, tq : tq + BANK].rearrange("p (j s) -> p j s", s=PACK),
                 op=ALU.mult,
             )
-            tmp[i] = t
+            decayed[i] = product
 
-        def s_swish(i):
+        def scalar_swish(i, slot):
             b, gq, gk, tq = step_ids(i)
             key = ("g", b, gq, gk)
             if tq == 0:
-                new_grp(key)
-            nc.scalar.activation(out=grp[key][:, tq * 512 : (tq + 1) * 512], in_=tmp[i][:], func=ACT.Silu)
+                new_grouped(key)
+            nc.scalar.activation(out=grouped[key][:, tq * BANK : (tq + 1) * BANK], in_=decayed[i][:], func=ACT.Silu)
+            if i >= LAST_ROUND:
+                later(slot + 1, quantise_query_block, (key, tq))
+            elif tq == PACK - 1:
+                later(slot + 1, quantise, key)
 
-        def pe_out(b, gq, tq):
-            bank = fx_bank()
-            for gk in range(2):
-                mx(bank[:], codes[("g", b, gq, gk)], tq * P, codes[("v", b, gk)], 0, 512, start=(gk == 0), stop=(gk == 1))
-            return [("O", (b, gq), tq, bank)]
-
-        stage = {}
-
-        def exit_out(eng, key, tq, bank):
-            if tq == 0:
-                stage[key] = work.tile([P, 2048], F32, name="ost", tag="ost", bufs=3)
-            drain(eng, stage[key][:, tq * 512 : (tq + 1) * 512], bank[:])
-            b, gq = key
-            if (b, gq) == (B - 1, 1):
-                view = out[b].rearrange("(g j t) h -> g t j h", g=2, j=P, t=4)
-                nc.sync.dma_start(out=view[gq, tq], in_=stage[key][:, tq * 512 : (tq + 1) * 512])
-            elif tq == 3:
-                view = out[b].rearrange("(g j t) h -> g j (t h)", g=2, j=P, t=4)
-                nc.sync.dma_start(out=view[gq], in_=stage[key][:])
-
-        prep = []
-        for b in range(B):
-            for name, g in (("k", 0), ("q", 0), ("k", 1), ("q", 1), ("x", 0), ("x", 1)):
-                prep.append(("T", name, b, g))
-            for g in range(2):
-                for hb in range(4):
-                    prep.append(("V", b, g, hb))
-        pending = []
-        state = {"prep": 0, "sc": 0, "outs": 0, "pending": 0, "due": []}
-
-        def w_regroup(arg):
-            new_grp(("w",))
+        def regroup_w(unused):
+            new_grouped(("w",))
             nc.vector.tensor_copy(
-                out=grp[("w",)][:].rearrange("p (c t) -> p c t", t=4),
-                in_=w_raw[:].rearrange("p (t c) -> p c t", t=4),
+                out=grouped[("w",)][:].rearrange("p (c t) -> p c t", t=PACK),
+                in_=w_rows[:].rearrange("p (t c) -> p c t", t=PACK),
             )
 
-        state["due"].append((0, w_regroup, None))
-        state["due"].append((1, quantise, ("w",)))
+        inputs_stream = []
+        for b in range(B):
+            for name, g in (("k", 0), ("q", 0), ("k", 1), ("q", 1), ("x", 0), ("x", 1)):
+                inputs_stream.append(("transposes", name, b, g))
+            for g in range(2):
+                for part in range(PACK):
+                    inputs_stream.append(("v", b, g, part))
+        filled = []
+        at = {"inputs": 0, "scores": 0, "out": 0, "emptied": 0}
+        todo = {"vector": []}
 
-        def next_side(slot):
-            room = NFX - (len(pending) - state["pending"])
-            if state["outs"] < len(outs) and room >= 1:
-                b, gq, tq = outs[state["outs"]]
-                if ("v", b, 0) in have and ("v", b, 1) in have:
-                    state["outs"] += 1
-                    return pe_out(b, gq, tq)
-            if state["prep"] < len(prep):
-                job = prep[state["prep"]]
-                if (
-                    job[0] == "T"
-                    and room >= 2
-                    and slot >= 16 * (job[2] - 1) - 8
-                    and slot >= GATE_STEP * place[(job[1], job[2], job[3])] - GATE_BASE
-                ):
-                    state["prep"] += 1
-                    return pe_transposes(job[1], job[2], job[3])
-                if job[0] == "V" and room >= 1 and ("x", job[1], job[2]) in have and ("w",) in have:
-                    state["prep"] += 1
-                    return pe_v(job[1], job[2], job[3])
+        def later(slot, function, argument):
+            todo["vector"].append((slot, function, argument))
+
+        later(0, regroup_w, None)
+        later(1, quantise, ("w",))
+
+        def tensor_scores_ahead(slot):
+            while at["scores"] < STEPS and at["scores"] <= slot + SCORES_AHEAD:
+                b, gq, gk, tq = step_ids(at["scores"])
+                if ("k", b, gk) not in quantised or ("q", b, gq) not in quantised:
+                    break
+                tensor_scores(at["scores"])
+                at["scores"] += 1
+
+        def tensor_side_next(slot):
+            room = SIDE_BANKS - (len(filled) - at["emptied"])
+            if at["out"] < len(out_ready) and room >= 1:
+                b, gq, tq = out_ready[at["out"]]
+                if ("v", b, 0) in quantised and ("v", b, 1) in quantised:
+                    at["out"] += 1
+                    return tensor_out(b, gq, tq)
+            if at["inputs"] < len(inputs_stream):
+                job = inputs_stream[at["inputs"]]
+                if job[0] == "transposes" and room >= 2 and slot >= LOAD_PACE * place[job[1:]] - LOAD_LEAD:
+                    at["inputs"] += 1
+                    return tensor_transposes(job[1], job[2], job[3])
+                if job[0] == "v" and room >= 1 and ("x", job[1], job[2]) in quantised and ("w",) in quantised:
+                    at["inputs"] += 1
+                    return tensor_v(job[1], job[2], job[3])
             return None
 
-        def side_exit(eng, slot):
-            if state["pending"] == len(pending):
+        def tensor_side(slot):
+            while True:
+                banks = tensor_side_next(slot)
+                if banks is None:
+                    break
+                filled.extend(banks)
+
+        def empty_next(engine, slot):
+            if at["emptied"] == len(filled):
                 return
-            kind, key, part, bank = pending[state["pending"]]
-            state["pending"] += 1
-            if kind == "T":
-                exit_transposes(eng, key, part, bank)
+            kind, key, part, bank = filled[at["emptied"]]
+            at["emptied"] += 1
+            if kind == "transposes":
+                empty_transposes(engine, key, part, bank)
                 if part == 1:
-                    state["due"].append((slot + 1, quantise, key))
-            elif kind == "V":
-                exit_v(eng, key, part, bank)
-                if part == 3:
-                    state["due"].append((slot + 1, quantise, key))
+                    later(slot + 1, quantise, key)
+            elif kind == "v":
+                empty_v(engine, key, part, bank)
+                if part == PACK - 1:
+                    later(slot + 1, quantise, key)
             else:
-                exit_out(eng, key, part, bank)
+                if key == (B - 1, 1):
+                    engine = "vector" if part % 2 == 0 else "scalar"
+                empty_out(engine, key, part, bank)
 
         def vector_due(slot):
-            now = [item for item in state["due"] if item[0] <= slot]
-            state["due"] = [item for item in state["due"] if item[0] > slot]
-            for item in now:
+            due = [item for item in todo["vector"] if item[0] <= slot]
+            todo["vector"] = [item for item in todo["vector"] if item[0] > slot]
+            for item in due:
                 item[1](item[2])
 
-        def swish_of(i, slot):
-            s_swish(i)
-            b, gq, gk, tq = step_ids(i)
-            if i >= FINE_FROM:
-                state["due"].append((slot + 1, quantise_block, (("g", b, gq, gk), tq)))
-            elif tq == 3:
-                state["due"].append((slot + 1, quantise, ("g", b, gq, gk)))
-
-        slot = -2
+        slot = FIRST_SLOT
         while True:
-            while state["sc"] < NSTEP and state["sc"] <= slot + 2:
-                b, gq, gk, tq = step_ids(state["sc"])
-                if ("k", b, gk) not in have or ("q", b, gq) not in have:
-                    break
-                pe_scores(state["sc"])
-                state["sc"] += 1
-            while True:
-                got = next_side(slot)
-                if got is None:
-                    break
-                pending.extend(got)
-            if 0 <= slot < NSTEP:
-                assert state["sc"] > slot, "scores of step %d are late" % slot
+            tensor_scores_ahead(slot)
+            tensor_side(slot)
+            if 0 <= slot < STEPS:
+                assert at["scores"] > slot, "the scores of step %d have no operands yet" % slot
                 if slot >= 1:
-                    swish_of(slot - 1, slot)
-                side_exit("S", slot)
+                    scalar_swish(slot - 1, slot)
+                empty_next("scalar", slot)
                 if slot % 8 in S_TWICE:
-                    side_exit("S", slot)
-                v_decay(slot)
+                    empty_next("scalar", slot)
+                vector_decay(slot)
                 if slot % 8 in V_SIDE:
-                    side_exit("V", slot)
+                    empty_next("vector", slot)
                 vector_due(slot)
             else:
                 vector_due(slot)
-                if slot == NSTEP:
-                    swish_of(slot - 1, slot)
-                for eng in ("S", "V", "S", "V"):
-                    side_exit(eng, slot)
+                if slot == STEPS:
+                    scalar_swish(slot - 1, slot)
+                for engine in ("scalar", "vector", "scalar", "vector"):
+                    empty_next(engine, slot)
             slot += 1
-            idle = state["pending"] == len(pending) and not state["due"] and state["outs"] == len(outs)
-            if slot > NSTEP and idle and state["prep"] == len(prep):
+            side_done = at["inputs"] == len(inputs_stream) and at["out"] == len(out_ready) and at["emptied"] == len(filled)
+            if slot > STEPS and side_done and not todo["vector"]:
                 break

@@ -31,6 +31,7 @@ S_TWICE = (2, 5, 7)
 V_SIDE = (1, 4, 7)
 
 LOAD_PACE, LOAD_LEAD = 1.25, 4.0
+TRANSPOSE_PACE, TRANSPOSE_LEAD = 16.0 / 6.0, 11.0
 HALVED_LOADS = 2
 FIRST_SLOT = -2
 LAST_ROUND = STEPS - PACK
@@ -288,15 +289,16 @@ def tile_simpleretention_pa_t_kernel(tc, q, k, x, w_v, out):
                 in_=w_rows[:].rearrange("p (t c) -> p c t", t=PACK),
             )
 
-        inputs_stream = []
+        to_transpose = []
+        v_banks = []
         for b in range(B):
             for name, g in (("k", 0), ("q", 0), ("k", 1), ("q", 1), ("x", 0), ("x", 1)):
-                inputs_stream.append(("transposes", name, b, g))
+                to_transpose.append((name, b, g))
             for g in range(2):
                 for part in range(PACK):
-                    inputs_stream.append(("v", b, g, part))
+                    v_banks.append((b, g, part))
         filled = []
-        at = {"inputs": 0, "scores": 0, "out": 0, "emptied": 0}
+        at = {"transposes": 0, "v": 0, "scores": 0, "out": 0, "emptied": 0}
         todo = {"vector": []}
 
         def later(slot, function, argument):
@@ -315,19 +317,22 @@ def tile_simpleretention_pa_t_kernel(tc, q, k, x, w_v, out):
 
         def tensor_side_next(slot):
             room = SIDE_BANKS - (len(filled) - at["emptied"])
+            n = at["transposes"]
+            if n < len(to_transpose) and room >= 2:
+                tile = to_transpose[n]
+                if slot >= LOAD_PACE * place[tile] - LOAD_LEAD and slot >= TRANSPOSE_PACE * n - TRANSPOSE_LEAD:
+                    at["transposes"] += 1
+                    return tensor_transposes(tile[0], tile[1], tile[2])
             if at["out"] < len(out_ready) and room >= 1:
                 b, gq, tq = out_ready[at["out"]]
                 if ("v", b, 0) in quantised and ("v", b, 1) in quantised:
                     at["out"] += 1
                     return tensor_out(b, gq, tq)
-            if at["inputs"] < len(inputs_stream):
-                job = inputs_stream[at["inputs"]]
-                if job[0] == "transposes" and room >= 2 and slot >= LOAD_PACE * place[job[1:]] - LOAD_LEAD:
-                    at["inputs"] += 1
-                    return tensor_transposes(job[1], job[2], job[3])
-                if job[0] == "v" and room >= 1 and ("x", job[1], job[2]) in quantised and ("w",) in quantised:
-                    at["inputs"] += 1
-                    return tensor_v(job[1], job[2], job[3])
+            if at["v"] < len(v_banks) and room >= 1:
+                b, g, part = v_banks[at["v"]]
+                if ("x", b, g) in quantised and ("w",) in quantised:
+                    at["v"] += 1
+                    return tensor_v(b, g, part)
             return None
 
         def tensor_side(slot):
@@ -383,6 +388,11 @@ def tile_simpleretention_pa_t_kernel(tc, q, k, x, w_v, out):
                 for engine in ("scalar", "vector", "scalar", "vector"):
                     empty_next(engine, slot)
             slot += 1
-            side_done = at["inputs"] == len(inputs_stream) and at["out"] == len(out_ready) and at["emptied"] == len(filled)
+            side_done = (
+                at["transposes"] == len(to_transpose)
+                and at["v"] == len(v_banks)
+                and at["out"] == len(out_ready)
+                and at["emptied"] == len(filled)
+            )
             if slot > STEPS and side_done and not todo["vector"]:
                 break

@@ -16,22 +16,23 @@ GAMMA = 0.96875
 FLOPS = 2 * B * S * H * H + 4 * B * S * S * H
 
 P = 128
+QUAD = 32
 PACK = 4
 PASS = P * PACK
 BANK = 512
 GROUP = PASS * PACK
 
-STEPS = B * 2 * 2 * PACK
-STEPS_PER_SEQ = STEPS // B
+ROUND = 2 * PACK
+STEPS_PER_SEQ = 2 * ROUND
+STEPS = B * STEPS_PER_SEQ
 SCORE_BANKS = 3
 SIDE_BANKS = 5
 SCORES_AHEAD = 2
 
-S_TWICE = (2, 5, 7)
-V_SIDE = (1, 4, 7)
+S_TWICE = (2, 5, 7, 10, 14)
+V_SIDE = (1, 4, 7, 9, 11, 13, 15)
 
 LOAD_PACE, LOAD_LEAD = 1.25, 4.0
-TRANSPOSE_PACE, TRANSPOSE_LEAD = 16.0 / 6.0, 11.0
 HALVED_LOADS = 2
 FIRST_SLOT = -2
 LAST_ROUND = STEPS - PACK
@@ -60,7 +61,7 @@ def tile_simpleretention_pa_t_kernel(tc, q, k, x, w_v, out):
         place = {}
 
         def load(name, b, g):
-            place[(name, b, g)] = len(place) + (1 if len(place) >= 4 else 0)
+            place[(name, b, g)] = len(place) + (1 if len(place) >= 2 else 0)
             tile = loads.tile([P, GROUP], BF16, name="in_" + name, tag="in_" + name, bufs=LOAD_BUFS)
             rows = inputs[name][b].rearrange("(g p t) h -> g p (t h)", g=2, p=P, t=PACK)[g]
             if len(place) <= HALVED_LOADS:
@@ -72,15 +73,15 @@ def tile_simpleretention_pa_t_kernel(tc, q, k, x, w_v, out):
 
         w_rows = const.tile([P, GROUP], BF16, name="w_rows")
         for b in range(B):
-            for name, g in (("k", 0), ("q", 0), ("k", 1), ("q", 1)):
-                load(name, b, g)
+            load("k", b, 0)
+            load("q", b, 0)
             if b == 0:
                 nc.sync.dma_start(
                     out=w_rows[:].rearrange("p (u f) -> p u f", u=2),
                     in_=w_v.rearrange("(u p e) c -> p u (e c)", u=2, p=P, e=2),
                 )
-            load("x", b, 0)
-            load("x", b, 1)
+            for name, g in (("k", 1), ("q", 1), ("x", 0), ("x", 1)):
+                load(name, b, g)
 
         ident = const.tile([P, P], F32, name="ident")
         make_identity(nc, ident[:])
@@ -99,23 +100,38 @@ def tile_simpleretention_pa_t_kernel(tc, q, k, x, w_v, out):
                 scalar1=GAMMA**done,
             )
             done *= 2
-        rows4 = const.tile([P, 2 * P], F32, name="rows4")
-        nc.vector.tensor_copy(
-            out=rows4[:, 0:P], in_=rising[:, 0:PASS].rearrange("p (a f) -> p a f", f=PACK)[:, :, 0]
-        )
-        nc.vector.tensor_copy(
-            out=rows4[:, P : 2 * P], in_=falling[:, PACK:TABLE].rearrange("p (a f) -> p a f", f=PACK)[:, :, PACK - 1]
-        )
-        turned = psum.tile([P, BANK], F32, name="side", tag="side", bufs=SIDE_BANKS)
-        nc.tensor.transpose(out=turned[:, 0:P], in_=rows4[:, 0:P], identity=ident[:])
-        nc.tensor.transpose(out=turned[:, P : 2 * P], in_=rows4[:, P : 2 * P], identity=ident[:])
-        by_part = const.tile([P, 2], F32, name="by_part")
-        nc.vector.tensor_copy(out=by_part[:], in_=turned[:, 0 : 2 * P].rearrange("p (a c) -> p a c", a=2)[:, :, 0])
+        seeds = const.tile([P, 2 * QUAD], F32, name="seeds", align_bytes=64)
+        nc.vector.memset(seeds[:, 0:1], 1.0)
+        nc.vector.memset(seeds[:, 2 * QUAD - 1 : 2 * QUAD], 1.0)
+        done = 1
+        while done < QUAD:
+            nc.vector.tensor_scalar_mul(out=seeds[:, done : 2 * done], in0=seeds[:, 0:done], scalar1=GAMMA ** (4 * done))
+            nc.vector.tensor_scalar_mul(
+                out=seeds[:, 2 * QUAD - 2 * done : 2 * QUAD - done],
+                in0=seeds[:, 2 * QUAD - done : 2 * QUAD],
+                scalar1=GAMMA ** (4 * done),
+            )
+            done *= 2
+        for group in range(P // QUAD):
+            lanes = slice(group * QUAD, (group + 1) * QUAD)
+            if group > 0:
+                nc.vector.tensor_scalar_mul(
+                    out=seeds[lanes, 0:QUAD], in0=seeds[lanes, 0:QUAD], scalar1=GAMMA ** (4 * QUAD * group)
+                )
+            if group < P // QUAD - 1:
+                nc.vector.tensor_scalar_mul(
+                    out=seeds[lanes, QUAD : 2 * QUAD],
+                    in0=seeds[lanes, QUAD : 2 * QUAD],
+                    scalar1=GAMMA ** (4 * QUAD * (P // QUAD - 1 - group)),
+                )
+        by_part = const.tile([P, 2 * QUAD], F32, name="by_part", align_bytes=64)
+        nc.vector.transpose(out=by_part[:, 0:QUAD], in_=seeds[:, 0:QUAD])
+        nc.vector.transpose(out=by_part[:, QUAD : 2 * QUAD], in_=seeds[:, QUAD : 2 * QUAD])
         above = const.tile([P, TABLE], F32, name="above")
         below = const.tile([P, TABLE], F32, name="below")
         level = const.tile([P, TABLE], F32, name="level")
         nc.vector.tensor_scalar_mul(out=above[:, 0:WINDOWS], in0=falling[:, 0:WINDOWS], scalar1=by_part[:, 0:1])
-        nc.vector.tensor_scalar_mul(out=below[:, 0:WINDOWS], in0=rising[:, 1 : WINDOWS + 1], scalar1=by_part[:, 1:2])
+        nc.vector.tensor_scalar_mul(out=below[:, 0:WINDOWS], in0=rising[:, 1 : WINDOWS + 1], scalar1=by_part[:, QUAD : QUAD + 1])
         nc.vector.tensor_tensor(out=level[:, 0:WINDOWS], in0=above[:, 0:WINDOWS], in1=below[:, 0:WINDOWS], op=ALU.min)
         nc.vector.tensor_scalar_mul(out=level[:, 0:WINDOWS], in0=level[:, 0:WINDOWS], scalar1=GAMMA ** (-PASS))
         decay = {1: above, -1: below, 0: level}
@@ -158,6 +174,20 @@ def tile_simpleretention_pa_t_kernel(tc, q, k, x, w_v, out):
                 for tq in range(PACK):
                     out_ready.append((key[1], key[2], tq))
 
+        def quantise_bank(key_and_part):
+            key, part = key_and_part
+            if part == 0:
+                new_codes(key)
+            words, scales = codes[key]
+            nc.vector.quantize_mx(
+                out=words[:, part * 2 * P : (part + 1) * 2 * P].bitcast(FP8X4),
+                scales=scales[:, part * 2 * P : (part + 1) * 2 * P],
+                in_=grouped[key][:, part * 2 * BANK : (part + 1) * 2 * BANK],
+            )
+            quantised.add((key, part))
+            if part == 1:
+                quantised.add(key)
+
         def quantise_query_block(key_and_block):
             key, tq = key_and_block
             if tq == 0:
@@ -194,11 +224,14 @@ def tile_simpleretention_pa_t_kernel(tc, q, k, x, w_v, out):
             banks = []
             for part in range(2):
                 bank = side_bank()
-                for c in range(4):
-                    first = (2 * part + c // 2) * (H // 2) + (c % 2) * P
-                    nc.tensor.transpose(
-                        out=bank[:, c * P : (c + 1) * P], in_=words[:, first : first + P], identity=ident[:]
-                    )
+                for a in range(2):
+                    for u in range(2):
+                        first = (2 * part + a) * (H // 2) + u * P
+                        nc.tensor.transpose(
+                            out=bank[:, (2 * a + u) * P : (2 * a + u + 1) * P],
+                            in_=words[:, first : first + P],
+                            identity=ident[:],
+                        )
                 banks.append(("transposes", (name, b, g), part, bank))
             return banks
 
@@ -249,7 +282,7 @@ def tile_simpleretention_pa_t_kernel(tc, q, k, x, w_v, out):
                 nc.sync.dma_start(out=rows[gq], in_=staged[key][:])
 
         def step_ids(i):
-            return i // STEPS_PER_SEQ, (i % STEPS_PER_SEQ) // 8, (i % 8) // PACK, i % PACK
+            return i // STEPS_PER_SEQ, (i % STEPS_PER_SEQ) // ROUND, (i % ROUND) // PACK, i % PACK
 
         score_bank = {}
         decayed = {}
@@ -282,57 +315,52 @@ def tile_simpleretention_pa_t_kernel(tc, q, k, x, w_v, out):
             elif tq == PACK - 1:
                 later(slot + 1, quantise, key)
 
-        def regroup_w(unused):
-            new_grouped(("w",))
-            nc.vector.tensor_copy(
-                out=grouped[("w",)][:].rearrange("p (c t) -> p c t", t=PACK),
+        def regroup_w(key):
+            new_grouped(key)
+            nc.scalar.copy(
+                out=grouped[key][:].rearrange("p (c t) -> p c t", t=PACK),
                 in_=w_rows[:].rearrange("p (t c) -> p c t", t=PACK),
             )
 
-        to_transpose = []
-        v_banks = []
+        inputs_stream = []
         for b in range(B):
             for name, g in (("k", 0), ("q", 0), ("k", 1), ("q", 1), ("x", 0), ("x", 1)):
-                to_transpose.append((name, b, g))
+                inputs_stream.append(("transposes", name, b, g))
             for g in range(2):
                 for part in range(PACK):
-                    v_banks.append((b, g, part))
+                    inputs_stream.append(("v", b, g, part))
         filled = []
-        at = {"transposes": 0, "v": 0, "scores": 0, "out": 0, "emptied": 0}
+        at = {"inputs": 0, "scores": 0, "out": 0, "emptied": 0}
         todo = {"vector": []}
 
         def later(slot, function, argument):
             todo["vector"].append((slot, function, argument))
 
-        later(0, regroup_w, None)
         later(1, quantise, ("w",))
 
         def tensor_scores_ahead(slot):
             while at["scores"] < STEPS and at["scores"] <= slot + SCORES_AHEAD:
                 b, gq, gk, tq = step_ids(at["scores"])
-                if ("k", b, gk) not in quantised or ("q", b, gq) not in quantised:
+                if ("k", b, gk) not in quantised or (("q", b, gq), tq // 2) not in quantised:
                     break
                 tensor_scores(at["scores"])
                 at["scores"] += 1
 
         def tensor_side_next(slot):
             room = SIDE_BANKS - (len(filled) - at["emptied"])
-            n = at["transposes"]
-            if n < len(to_transpose) and room >= 2:
-                tile = to_transpose[n]
-                if slot >= LOAD_PACE * place[tile] - LOAD_LEAD and slot >= TRANSPOSE_PACE * n - TRANSPOSE_LEAD:
-                    at["transposes"] += 1
-                    return tensor_transposes(tile[0], tile[1], tile[2])
             if at["out"] < len(out_ready) and room >= 1:
                 b, gq, tq = out_ready[at["out"]]
                 if ("v", b, 0) in quantised and ("v", b, 1) in quantised:
                     at["out"] += 1
                     return tensor_out(b, gq, tq)
-            if at["v"] < len(v_banks) and room >= 1:
-                b, g, part = v_banks[at["v"]]
-                if ("x", b, g) in quantised and ("w",) in quantised:
-                    at["v"] += 1
-                    return tensor_v(b, g, part)
+            if at["inputs"] < len(inputs_stream):
+                job = inputs_stream[at["inputs"]]
+                if job[0] == "transposes" and room >= 2 and slot >= LOAD_PACE * place[job[1:]] - LOAD_LEAD:
+                    at["inputs"] += 1
+                    return tensor_transposes(job[1], job[2], job[3])
+                if job[0] == "v" and room >= 1 and ("x", job[1], job[2]) in quantised and ("w",) in quantised:
+                    at["inputs"] += 1
+                    return tensor_v(job[1], job[2], job[3])
             return None
 
         def tensor_side(slot):
@@ -349,8 +377,7 @@ def tile_simpleretention_pa_t_kernel(tc, q, k, x, w_v, out):
             at["emptied"] += 1
             if kind == "transposes":
                 empty_transposes(engine, key, part, bank)
-                if part == 1:
-                    later(slot + 1, quantise, key)
+                later(slot + 1, quantise_bank, (key, part))
             elif kind == "v":
                 empty_v(engine, key, part, bank)
                 if part == PACK - 1:
@@ -372,13 +399,15 @@ def tile_simpleretention_pa_t_kernel(tc, q, k, x, w_v, out):
             tensor_side(slot)
             if 0 <= slot < STEPS:
                 assert at["scores"] > slot, "the scores of step %d have no operands yet" % slot
+                if slot == 0:
+                    regroup_w(("w",))
                 if slot >= 1:
                     scalar_swish(slot - 1, slot)
                 empty_next("scalar", slot)
-                if slot % 8 in S_TWICE:
+                if slot % STEPS_PER_SEQ in S_TWICE:
                     empty_next("scalar", slot)
                 vector_decay(slot)
-                if slot % 8 in V_SIDE:
+                if slot % STEPS_PER_SEQ in V_SIDE:
                     empty_next("vector", slot)
                 vector_due(slot)
             else:
@@ -388,11 +417,6 @@ def tile_simpleretention_pa_t_kernel(tc, q, k, x, w_v, out):
                 for engine in ("scalar", "vector", "scalar", "vector"):
                     empty_next(engine, slot)
             slot += 1
-            side_done = (
-                at["transposes"] == len(to_transpose)
-                and at["v"] == len(v_banks)
-                and at["out"] == len(out_ready)
-                and at["emptied"] == len(filled)
-            )
+            side_done = at["inputs"] == len(inputs_stream) and at["out"] == len(out_ready) and at["emptied"] == len(filled)
             if slot > STEPS and side_done and not todo["vector"]:
                 break

@@ -16,7 +16,6 @@ GAMMA = 0.96875
 FLOPS = 2 * B * S * H * H + 4 * B * S * S * H
 
 P = 128
-QUAD = 32
 PACK = 4
 PASS = P * PACK
 BANK = 512
@@ -37,7 +36,6 @@ HALVED_LOADS = 2
 FIRST_SLOT = -2
 LAST_ROUND = STEPS - PACK
 
-TABLE = PASS + PACK
 WINDOWS = BANK + PACK - 1
 
 LOAD_BUFS = 6
@@ -61,7 +59,7 @@ def tile_simpleretention_pa_t_kernel(tc, q, k, x, w_v, out):
         place = {}
 
         def load(name, b, g):
-            place[(name, b, g)] = len(place) + (1 if len(place) >= 2 else 0)
+            place[(name, b, g)] = len(place) + (1 if len(place) >= 6 else 0)
             tile = loads.tile([P, GROUP], BF16, name="in_" + name, tag="in_" + name, bufs=LOAD_BUFS)
             rows = inputs[name][b].rearrange("(g p t) h -> g p (t h)", g=2, p=P, t=PACK)[g]
             if len(place) <= HALVED_LOADS:
@@ -75,65 +73,43 @@ def tile_simpleretention_pa_t_kernel(tc, q, k, x, w_v, out):
         for b in range(B):
             load("k", b, 0)
             load("q", b, 0)
+            for name, g in (("k", 1), ("q", 1), ("x", 0), ("x", 1)):
+                load(name, b, g)
             if b == 0:
                 nc.sync.dma_start(
                     out=w_rows[:].rearrange("p (u f) -> p u f", u=2),
                     in_=w_v.rearrange("(u p e) c -> p u (e c)", u=2, p=P, e=2),
                 )
-            for name, g in (("k", 1), ("q", 1), ("x", 0), ("x", 1)):
-                load(name, b, g)
+
+        base = const.tile([P, 2], F32, name="base")
+        exponents = const.tile([P, 2], F32, name="exponents")
+        seeds = const.tile([P, 2], F32, name="seeds")
+        nc.gpsimd.memset(base[:], GAMMA)
+        nc.gpsimd.iota(
+            exponents[:, 0:1], [[1, 1]], base=1, channel_multiplier=PACK, allow_small_or_imprecise_dtypes=True
+        )
+        nc.gpsimd.iota(
+            exponents[:, 1:2], [[1, 1]], base=PASS - 3, channel_multiplier=-PACK, allow_small_or_imprecise_dtypes=True
+        )
+        nc.gpsimd.tensor_tensor(out=seeds[:], in0=base[:], in1=exponents[:], op=ALU.pow)
 
         ident = const.tile([P, P], F32, name="ident")
         make_identity(nc, ident[:])
 
-        rising = const.tile([P, TABLE], F32, name="rising")
-        falling = const.tile([P, TABLE], F32, name="falling")
+        rising = const.tile([P, WINDOWS], F32, name="rising")
         nc.vector.memset(rising[:, 0:1], 1.0)
-        nc.vector.memset(falling[:, TABLE - 1 : TABLE], 1.0)
         done = 1
-        while done < TABLE:
-            more = min(done, TABLE - done)
+        while done < WINDOWS:
+            more = min(done, WINDOWS - done)
             nc.vector.tensor_scalar_mul(out=rising[:, done : done + more], in0=rising[:, 0:more], scalar1=GAMMA**done)
-            nc.vector.tensor_scalar_mul(
-                out=falling[:, TABLE - done - more : TABLE - done],
-                in0=falling[:, TABLE - more : TABLE],
-                scalar1=GAMMA**done,
-            )
             done *= 2
-        seeds = const.tile([P, 2 * QUAD], F32, name="seeds", align_bytes=64)
-        nc.vector.memset(seeds[:, 0:1], 1.0)
-        nc.vector.memset(seeds[:, 2 * QUAD - 1 : 2 * QUAD], 1.0)
-        done = 1
-        while done < QUAD:
-            nc.vector.tensor_scalar_mul(out=seeds[:, done : 2 * done], in0=seeds[:, 0:done], scalar1=GAMMA ** (4 * done))
-            nc.vector.tensor_scalar_mul(
-                out=seeds[:, 2 * QUAD - 2 * done : 2 * QUAD - done],
-                in0=seeds[:, 2 * QUAD - done : 2 * QUAD],
-                scalar1=GAMMA ** (4 * done),
-            )
-            done *= 2
-        for group in range(P // QUAD):
-            lanes = slice(group * QUAD, (group + 1) * QUAD)
-            if group > 0:
-                nc.vector.tensor_scalar_mul(
-                    out=seeds[lanes, 0:QUAD], in0=seeds[lanes, 0:QUAD], scalar1=GAMMA ** (4 * QUAD * group)
-                )
-            if group < P // QUAD - 1:
-                nc.vector.tensor_scalar_mul(
-                    out=seeds[lanes, QUAD : 2 * QUAD],
-                    in0=seeds[lanes, QUAD : 2 * QUAD],
-                    scalar1=GAMMA ** (4 * QUAD * (P // QUAD - 1 - group)),
-                )
-        by_part = const.tile([P, 2 * QUAD], F32, name="by_part", align_bytes=64)
-        nc.vector.transpose(out=by_part[:, 0:QUAD], in_=seeds[:, 0:QUAD])
-        nc.vector.transpose(out=by_part[:, QUAD : 2 * QUAD], in_=seeds[:, QUAD : 2 * QUAD])
-        above = const.tile([P, TABLE], F32, name="above")
-        below = const.tile([P, TABLE], F32, name="below")
-        level = const.tile([P, TABLE], F32, name="level")
-        nc.vector.tensor_scalar_mul(out=above[:, 0:WINDOWS], in0=falling[:, 0:WINDOWS], scalar1=by_part[:, 0:1])
-        nc.vector.tensor_scalar_mul(out=below[:, 0:WINDOWS], in0=rising[:, 1 : WINDOWS + 1], scalar1=by_part[:, QUAD : QUAD + 1])
-        nc.vector.tensor_tensor(out=level[:, 0:WINDOWS], in0=above[:, 0:WINDOWS], in1=below[:, 0:WINDOWS], op=ALU.min)
-        nc.vector.tensor_scalar_mul(out=level[:, 0:WINDOWS], in0=level[:, 0:WINDOWS], scalar1=GAMMA ** (-PASS))
+        above = const.tile([P, WINDOWS], F32, name="above")
+        below = const.tile([P, WINDOWS], F32, name="below")
+        level = const.tile([P, WINDOWS], F32, name="level")
+        nc.vector.tensor_scalar_mul(out=above[:], in0=rising[:, ::-1], scalar1=seeds[:, 0:1])
+        nc.vector.tensor_scalar_mul(out=below[:], in0=rising[:], scalar1=seeds[:, 1:2])
+        nc.vector.tensor_tensor(out=level[:], in0=above[:], in1=below[:], op=ALU.min)
+        nc.vector.tensor_scalar_mul(out=level[:], in0=level[:], scalar1=GAMMA ** (-PASS))
         decay = {1: above, -1: below, 0: level}
 
         grouped = {}
@@ -317,10 +293,15 @@ def tile_simpleretention_pa_t_kernel(tc, q, k, x, w_v, out):
 
         def regroup_w(key):
             new_grouped(key)
-            nc.scalar.copy(
-                out=grouped[key][:].rearrange("p (c t) -> p c t", t=PACK),
-                in_=w_rows[:].rearrange("p (t c) -> p c t", t=PACK),
-            )
+            for part in range(PACK):
+                nc.gpsimd.tensor_scalar(
+                    out=grouped[key][:, part * BANK : (part + 1) * BANK].rearrange("p (c t) -> p c t", t=PACK),
+                    in0=w_rows[:].rearrange("p (t c) -> p c t", t=PACK)[:, part * P : (part + 1) * P, :],
+                    scalar1=1.0,
+                    scalar2=0.0,
+                    op0=ALU.mult,
+                    op1=ALU.add,
+                )
 
         inputs_stream = []
         for b in range(B):
@@ -336,7 +317,7 @@ def tile_simpleretention_pa_t_kernel(tc, q, k, x, w_v, out):
         def later(slot, function, argument):
             todo["vector"].append((slot, function, argument))
 
-        later(1, quantise, ("w",))
+        later(6, quantise, ("w",))
 
         def tensor_scores_ahead(slot):
             while at["scores"] < STEPS and at["scores"] <= slot + SCORES_AHEAD:

@@ -34,6 +34,7 @@ V_SIDE = (1, 4, 7, 9, 11, 13, 15)
 LOAD_PACE, LOAD_LEAD = 1.25, 4.0
 HALVED_LOADS = 2
 FIRST_SLOT = -2
+FIRST_PAIRED = ROUND
 LAST_ROUND = STEPS - PACK
 
 WINDOWS = BANK + PACK - 1
@@ -42,7 +43,7 @@ LOAD_BUFS = 6
 CODE_BUFS = {"k": 4, "q": 4, "x": 3, "v": 6, "g": 6, "w": 1}
 GROUPED_BUFS = 6
 SWISH_BUFS = 4
-DECAYED_BUFS = 6
+DECAYED_BUFS = 4
 STAGED_BUFS = 3
 
 
@@ -59,7 +60,7 @@ def tile_simpleretention_pa_t_kernel(tc, q, k, x, w_v, out):
         place = {}
 
         def load(name, b, g):
-            place[(name, b, g)] = len(place) + (1 if len(place) >= 6 else 0)
+            place[(name, b, g)] = len(place) + (1 if len(place) >= 7 else 0)
             tile = loads.tile([P, GROUP], BF16, name="in_" + name, tag="in_" + name, bufs=LOAD_BUFS)
             rows = inputs[name][b].rearrange("(g p t) h -> g p (t h)", g=2, p=P, t=PACK)[g]
             if len(place) <= HALVED_LOADS:
@@ -72,14 +73,13 @@ def tile_simpleretention_pa_t_kernel(tc, q, k, x, w_v, out):
         w_rows = const.tile([P, GROUP], BF16, name="w_rows")
         for b in range(B):
             load("k", b, 0)
-            load("q", b, 0)
-            for name, g in (("k", 1), ("q", 1), ("x", 0), ("x", 1)):
-                load(name, b, g)
-            if b == 0:
+            if b == 1:
                 nc.sync.dma_start(
                     out=w_rows[:].rearrange("p (u f) -> p u f", u=2),
                     in_=w_v.rearrange("(u p e) c -> p u (e c)", u=2, p=P, e=2),
                 )
+            for name, g in (("q", 0), ("k", 1), ("q", 1), ("x", 0), ("x", 1)):
+                load(name, b, g)
 
         base = const.tile([P, 2], F32, name="base")
         exponents = const.tile([P, 2], F32, name="exponents")
@@ -146,6 +146,9 @@ def tile_simpleretention_pa_t_kernel(tc, q, k, x, w_v, out):
             words, scales = codes[key]
             nc.vector.quantize_mx(out=words[:].bitcast(FP8X4), scales=scales[:], in_=grouped[key][:])
             quantised.add(key)
+            if key[0] == "q":
+                quantised.add((key, 0))
+                quantised.add((key, 1))
             if key[0] == "g" and key[3] == 1:
                 for tq in range(PACK):
                     out_ready.append((key[1], key[2], tq))
@@ -271,25 +274,38 @@ def tile_simpleretention_pa_t_kernel(tc, q, k, x, w_v, out):
 
         def vector_decay(i):
             b, gq, gk, tq = step_ids(i)
-            product = work.tile([P, BANK], F32, name="decayed", tag="decayed", bufs=DECAYED_BUFS)
+            if i % 2 == 0:
+                decayed[i // 2] = work.tile([P, 2 * BANK], F32, name="decayed", tag="decayed", bufs=DECAYED_BUFS)
+            half = slice((i % 2) * BANK, (i % 2 + 1) * BANK)
             nc.vector.tensor_tensor(
-                out=product[:].rearrange("p (j s) -> p j s", s=PACK),
+                out=decayed[i // 2][:, half].rearrange("p (j s) -> p j s", s=PACK),
                 in0=score_bank[i][:].rearrange("p (s j) -> p j s", s=PACK),
                 in1=decay[gk - gq][:, tq : tq + BANK].rearrange("p (j s) -> p j s", s=PACK),
                 op=ALU.mult,
             )
-            decayed[i] = product
 
         def scalar_swish(i, slot):
             b, gq, gk, tq = step_ids(i)
             key = ("g", b, gq, gk)
-            if tq == 0:
-                new_grouped(key)
-            nc.scalar.activation(out=grouped[key][:, tq * BANK : (tq + 1) * BANK], in_=decayed[i][:], func=ACT.Silu)
-            if i >= LAST_ROUND:
-                later(slot + 1, quantise_query_block, (key, tq))
-            elif tq == PACK - 1:
-                later(slot + 1, quantise, key)
+            if i >= LAST_ROUND or i < FIRST_PAIRED:
+                if tq == 0:
+                    new_grouped(key)
+                half = slice((i % 2) * BANK, (i % 2 + 1) * BANK)
+                nc.scalar.activation(
+                    out=grouped[key][:, tq * BANK : (tq + 1) * BANK], in_=decayed[i // 2][:, half], func=ACT.Silu
+                )
+                if i >= LAST_ROUND:
+                    later(slot + 1, quantise_query_block, (key, tq))
+                elif tq == PACK - 1:
+                    later(slot + 1, quantise, key)
+            elif i % 2 == 1:
+                if tq == 1:
+                    new_grouped(key)
+                nc.scalar.activation(
+                    out=grouped[key][:, (tq - 1) * BANK : (tq + 1) * BANK], in_=decayed[i // 2][:], func=ACT.Silu
+                )
+                if tq == PACK - 1:
+                    later(slot + 1, quantise, key)
 
         def regroup_w(key):
             new_grouped(key)
@@ -358,7 +374,10 @@ def tile_simpleretention_pa_t_kernel(tc, q, k, x, w_v, out):
             at["emptied"] += 1
             if kind == "transposes":
                 empty_transposes(engine, key, part, bank)
-                later(slot + 1, quantise_bank, (key, part))
+                if key[1] == 0:
+                    later(slot + 1, quantise_bank, (key, part))
+                elif part == 1:
+                    later(slot + 1, quantise, key)
             elif kind == "v":
                 empty_v(engine, key, part, bank)
                 if part == PACK - 1:

@@ -24,16 +24,34 @@ GROUP = PASS * PACK
 ROUND = 2 * PACK
 STEPS_PER_SEQ = 2 * ROUND
 STEPS = B * STEPS_PER_SEQ
-SCORE_BANKS = 3
-SIDE_BANKS = 5
+SCORE_BANKS = 4
+SIDE_BANKS = 4
 SCORES_AHEAD = 2
 
 S_TWICE = (2, 5, 7, 10, 14)
 V_SIDE = (1, 4, 7, 9, 11, 13, 15)
 
-LOAD_PACE, LOAD_LEAD = 1.25, 4.0
 HALVED_LOADS = 2
-FIRST_SLOT = -2
+G_LAG = 1
+T_LAG = 1
+EARLY_SWISH = 63
+ORDER = "SDEQ"
+FILL = {("k", 0): 5, ("q", 0): 2, ("k", 1): 2}
+HEAD_SCORES = -1
+FIRST_SLOT = -3
+TILES = ((("x", 0), -12), (("k", 0), -8), (("q", 0), -6), (("k", 1), -4), (("q", 1), 0), (("x", 1), 2))
+V_PARTS = (-7, 1, 6, 7)
+OUT_SLOTS = ((11, 14), (19, 21))
+HEAD_TILES = ((("k", 0), -3), (("q", 0), -2), (("k", 1), -1), (("q", 1), 0), (("x", 0), 1), (("x", 1), 2))
+HEAD_V = (5, 6, 7, 9)
+LAST_OUT = ((11, 12), (17, 18))
+TAIL = ("scalar", "vector", "scalar", "vector")
+HEAD_OUT = ((14, 15), (19, 21))
+SECOND_V = (-5, 1, 6, 7)
+FIRST_LOADS = (("k", 0), ("q", 0), ("k", 1), ("q", 1), ("x", 0), ("x", 1))
+NEXT_LOADS = (("x", 0), ("k", 0), ("q", 0), ("k", 1), ("q", 1), ("x", 1))
+W_SLOT = 4
+EMPTY = (("vector", "scalar"), ("scalar", "scalar"))
 FIRST_PAIRED = ROUND
 LAST_ROUND = STEPS - PACK
 
@@ -72,14 +90,20 @@ def tile_simpleretention_pa_t_kernel(tc, q, k, x, w_v, out):
 
         w_rows = const.tile([P, GROUP], BF16, name="w_rows")
         for b in range(B):
-            load("k", b, 0)
-            if b == 1:
+            for name, g in FIRST_LOADS if b == 0 else NEXT_LOADS:
+                load(name, b, g)
+            if b == 0:
                 nc.sync.dma_start(
                     out=w_rows[:].rearrange("p (u f) -> p u f", u=2),
                     in_=w_v.rearrange("(u p e) c -> p u (e c)", u=2, p=P, e=2),
                 )
-            for name, g in (("q", 0), ("k", 1), ("q", 1), ("x", 0), ("x", 1)):
-                load(name, b, g)
+
+        zeros = const.tile([P, BANK], BF16, name="zeros")
+        nc.vector.memset(zeros[:], 0.0)
+
+        def fill_clock(bank, count, width):
+            for step in range(count):
+                nc.tensor.matmul(out=bank[:, 0:width], lhsT=zeros[:, 0:P], rhs=zeros[:, 0:width], start=True, stop=True)
 
         base = const.tile([P, 2], F32, name="base")
         exponents = const.tile([P, 2], F32, name="exponents")
@@ -203,6 +227,8 @@ def tile_simpleretention_pa_t_kernel(tc, q, k, x, w_v, out):
             banks = []
             for part in range(2):
                 bank = side_bank()
+                if b == 0 and (name, g) in FILL and part == 0:
+                    fill_clock(bank, FILL[(name, g)], BANK)
                 for a in range(2):
                     for u in range(2):
                         first = (2 * part + a) * (H // 2) + u * P
@@ -297,7 +323,7 @@ def tile_simpleretention_pa_t_kernel(tc, q, k, x, w_v, out):
                 if i >= LAST_ROUND:
                     later(slot + 1, quantise_query_block, (key, tq))
                 elif tq == PACK - 1:
-                    later(slot + 1, quantise, key)
+                    later(slot + G_LAG, quantise, key)
             elif i % 2 == 1:
                 if tq == 1:
                     new_grouped(key)
@@ -305,7 +331,7 @@ def tile_simpleretention_pa_t_kernel(tc, q, k, x, w_v, out):
                     out=grouped[key][:, (tq - 1) * BANK : (tq + 1) * BANK], in_=decayed[i // 2][:], func=ACT.Silu
                 )
                 if tq == PACK - 1:
-                    later(slot + 1, quantise, key)
+                    later(slot + G_LAG, quantise, key)
 
         def regroup_w(key):
             new_grouped(key)
@@ -319,72 +345,60 @@ def tile_simpleretention_pa_t_kernel(tc, q, k, x, w_v, out):
                     op1=ALU.add,
                 )
 
-        inputs_stream = []
+        calendar = {}
+
+        def at_slot(slot, *jobs):
+            calendar.setdefault(slot, []).extend(jobs)
+
         for b in range(B):
-            for name, g in (("k", 0), ("q", 0), ("k", 1), ("q", 1), ("x", 0), ("x", 1)):
-                inputs_stream.append(("transposes", name, b, g))
+            first = b * STEPS_PER_SEQ
+            for (name, g), offset in HEAD_TILES if b == 0 else TILES:
+                at_slot(first + offset, ("transposes", name, b, g))
             for g in range(2):
                 for part in range(PACK):
-                    inputs_stream.append(("v", b, g, part))
+                    offset = (HEAD_V if b == 0 else SECOND_V if b == 1 else V_PARTS)[2 * g + part // 2]
+                    at_slot(first + offset, ("v", b, g, part))
+            for gq in range(2):
+                for tq in range(PACK):
+                    at_slot(first + (HEAD_OUT if b == 0 else LAST_OUT if b == B - 1 else OUT_SLOTS)[gq][tq // 2], ("out", b, gq, tq))
         filled = []
-        at = {"inputs": 0, "scores": 0, "out": 0, "emptied": 0}
         todo = {"vector": []}
 
         def later(slot, function, argument):
             todo["vector"].append((slot, function, argument))
 
-        later(6, quantise, ("w",))
-
-        def tensor_scores_ahead(slot):
-            while at["scores"] < STEPS and at["scores"] <= slot + SCORES_AHEAD:
-                b, gq, gk, tq = step_ids(at["scores"])
-                if ("k", b, gk) not in quantised or (("q", b, gq), tq // 2) not in quantised:
-                    break
-                tensor_scores(at["scores"])
-                at["scores"] += 1
-
-        def tensor_side_next(slot):
-            room = SIDE_BANKS - (len(filled) - at["emptied"])
-            if at["out"] < len(out_ready) and room >= 1:
-                b, gq, tq = out_ready[at["out"]]
-                if ("v", b, 0) in quantised and ("v", b, 1) in quantised:
-                    at["out"] += 1
-                    return tensor_out(b, gq, tq)
-            if at["inputs"] < len(inputs_stream):
-                job = inputs_stream[at["inputs"]]
-                if job[0] == "transposes" and room >= 2 and slot >= LOAD_PACE * place[job[1:]] - LOAD_LEAD:
-                    at["inputs"] += 1
-                    return tensor_transposes(job[1], job[2], job[3])
-                if job[0] == "v" and room >= 1 and ("x", job[1], job[2]) in quantised and ("w",) in quantised:
-                    at["inputs"] += 1
-                    return tensor_v(job[1], job[2], job[3])
-            return None
+        later(W_SLOT, quantise, ("w",))
+        last_slot = max(calendar)
 
         def tensor_side(slot):
-            while True:
-                banks = tensor_side_next(slot)
-                if banks is None:
-                    break
-                filled.extend(banks)
+            for job in calendar.get(slot, []):
+                if job[0] == "transposes":
+                    banks = tensor_transposes(job[1], job[2], job[3])
+                elif job[0] == "v":
+                    banks = tensor_v(job[1], job[2], job[3])
+                else:
+                    banks = tensor_out(job[1], job[2], job[3])
+                for item in banks:
+                    filled.append((slot, item[0], item[1], item[2], item[3]))
+            assert len(filled) <= SIDE_BANKS, "side banks at slot %d: %d" % (slot, len(filled))
 
-        def empty_next(engine, slot):
-            if at["emptied"] == len(filled):
+        def empty_next(engine, slot, lag):
+            if len(filled) == 0 or filled[0][0] > slot - lag:
                 return
-            kind, key, part, bank = filled[at["emptied"]]
-            at["emptied"] += 1
+            item = filled[0]
+            filled.remove(item)
+            kind, key, part, bank = item[1], item[2], item[3], item[4]
             if kind == "transposes":
                 empty_transposes(engine, key, part, bank)
                 if key[1] == 0:
                     later(slot + 1, quantise_bank, (key, part))
                 elif part == 1:
-                    later(slot + 1, quantise, key)
+                    later(slot + T_LAG, quantise, key)
             elif kind == "v":
                 empty_v(engine, key, part, bank)
                 if part == PACK - 1:
                     later(slot + 1, quantise, key)
             else:
-                if key == (B - 1, 1):
-                    engine = "vector" if part % 2 == 0 else "scalar"
                 empty_out(engine, key, part, bank)
 
         def vector_due(slot):
@@ -393,30 +407,36 @@ def tile_simpleretention_pa_t_kernel(tc, q, k, x, w_v, out):
             for item in due:
                 item[1](item[2])
 
-        slot = FIRST_SLOT
-        while True:
-            tensor_scores_ahead(slot)
+        ctx.enter_context(tc.manual_schedule())
+        regroup_w(("w",))
+        for slot in range(FIRST_SLOT, last_slot + 4):
+            i = slot % STEPS_PER_SEQ
+            if slot < 0 or slot >= STEPS:
+                if slot >= STEPS:
+                    vector_due(slot)
+                tensor_side(slot)
+                if slot + SCORES_AHEAD == 0:
+                    pass
+                for engine in TAIL if slot >= STEPS else ("scalar", "vector", "scalar", "vector"):
+                    empty_next(engine, slot, 0)
+                if slot < 0:
+                    vector_due(slot + 1)
+                if slot == -1:
+                    for step in range(SCORES_AHEAD):
+                        tensor_scores(step)
+                continue
+            if slot + SCORES_AHEAD < STEPS:
+                tensor_scores(slot + SCORES_AHEAD)
             tensor_side(slot)
-            if 0 <= slot < STEPS:
-                assert at["scores"] > slot, "the scores of step %d have no operands yet" % slot
-                if slot == 0:
-                    regroup_w(("w",))
-                if slot >= 1:
+            for piece in ORDER:
+                if piece == "S" and 1 <= slot <= EARLY_SWISH:
                     scalar_swish(slot - 1, slot)
-                empty_next("scalar", slot)
-                if slot % STEPS_PER_SEQ in S_TWICE:
-                    empty_next("scalar", slot)
-                vector_decay(slot)
-                if slot % STEPS_PER_SEQ in V_SIDE:
-                    empty_next("vector", slot)
-                vector_due(slot)
-            else:
-                vector_due(slot)
-                if slot == STEPS:
-                    scalar_swish(slot - 1, slot)
-                for engine in ("scalar", "vector", "scalar", "vector"):
-                    empty_next(engine, slot)
-            slot += 1
-            side_done = at["inputs"] == len(inputs_stream) and at["out"] == len(out_ready) and at["emptied"] == len(filled)
-            if slot > STEPS and side_done and not todo["vector"]:
-                break
+                elif piece == "D":
+                    vector_decay(slot)
+                    if slot >= EARLY_SWISH:
+                        scalar_swish(slot, slot)
+                elif piece == "E":
+                    for engine in EMPTY[i % len(EMPTY)]:
+                        empty_next(engine, slot, 1)
+                elif piece == "Q":
+                    vector_due(slot)

@@ -36,7 +36,7 @@ G_LAG = 1
 T_LAG = 1
 EARLY_SWISH = 63
 ORDER = "SDEQ"
-FILL = {("k", 0): 5, ("q", 0): 2, ("k", 1): 2}
+FILL = {("k", 0): 8, ("q", 0): 4, ("k", 1): 4}
 HEAD_SCORES = -1
 FIRST_SLOT = -3
 TILES = ((("x", 0), -12), (("k", 0), -8), (("q", 0), -6), (("k", 1), -4), (("q", 1), 0), (("x", 1), 2))
@@ -44,6 +44,7 @@ V_PARTS = (-7, 1, 6, 7)
 OUT_SLOTS = ((11, 14), (19, 21))
 HEAD_TILES = ((("k", 0), -3), (("q", 0), -2), (("k", 1), -1), (("q", 1), 0), (("x", 0), 1), (("x", 1), 2))
 HEAD_V = (5, 6, 7, 9)
+PRE = {-3: ("scalar", "vector"), -2: ("scalar", "vector"), -1: ("scalar", "scalar")}
 LAST_OUT = ((11, 12), (17, 18))
 TAIL = ("scalar", "vector", "scalar", "vector")
 HEAD_OUT = ((14, 15), (19, 21))
@@ -51,7 +52,7 @@ SECOND_V = (-5, 1, 6, 7)
 FIRST_LOADS = (("k", 0), ("q", 0), ("k", 1), ("q", 1), ("x", 0), ("x", 1))
 NEXT_LOADS = (("x", 0), ("k", 0), ("q", 0), ("k", 1), ("q", 1), ("x", 1))
 W_SLOT = 4
-EMPTY = (("vector", "scalar"), ("scalar", "scalar"))
+EMPTY = (("vector", "scalar"), ("scalar", "scalar"), ("vector", "scalar"), ("scalar", "scalar"), ("vector", "scalar"), ("scalar", "scalar"), ("vector", "scalar"), ("scalar", "scalar"), ("vector", "scalar"), ("scalar", "scalar"), ("vector", "scalar"), ("scalar", "scalar"), ("vector", "scalar"), ("scalar", "scalar"), ("vector", "scalar"), ("scalar", "vector"))
 FIRST_PAIRED = ROUND
 LAST_ROUND = STEPS - PACK
 
@@ -98,7 +99,7 @@ def tile_simpleretention_pa_t_kernel(tc, q, k, x, w_v, out):
                     in_=w_v.rearrange("(u p e) c -> p u (e c)", u=2, p=P, e=2),
                 )
 
-        zeros = const.tile([P, BANK], BF16, name="zeros")
+        zeros = const.tile([P, 2 * P], BF16, name="zeros")
         nc.vector.memset(zeros[:], 0.0)
 
         def fill_clock(bank, count, width):
@@ -110,30 +111,34 @@ def tile_simpleretention_pa_t_kernel(tc, q, k, x, w_v, out):
         seeds = const.tile([P, 2], F32, name="seeds")
         nc.gpsimd.memset(base[:], GAMMA)
         nc.gpsimd.iota(
-            exponents[:, 0:1], [[1, 1]], base=1, channel_multiplier=PACK, allow_small_or_imprecise_dtypes=True
+            exponents[:, 0:1], [[1, 1]], base=-PASS, channel_multiplier=PACK, allow_small_or_imprecise_dtypes=True
         )
         nc.gpsimd.iota(
-            exponents[:, 1:2], [[1, 1]], base=PASS - 3, channel_multiplier=-PACK, allow_small_or_imprecise_dtypes=True
+            exponents[:, 1:2], [[1, 1]], base=-4, channel_multiplier=-PACK, allow_small_or_imprecise_dtypes=True
         )
         nc.gpsimd.tensor_tensor(out=seeds[:], in0=base[:], in1=exponents[:], op=ALU.pow)
 
         ident = const.tile([P, P], F32, name="ident")
         make_identity(nc, ident[:])
 
+        gammas = const.tile([P, WINDOWS], F32, name="gammas")
         rising = const.tile([P, WINDOWS], F32, name="rising")
-        nc.vector.memset(rising[:, 0:1], 1.0)
-        done = 1
-        while done < WINDOWS:
-            more = min(done, WINDOWS - done)
-            nc.vector.tensor_scalar_mul(out=rising[:, done : done + more], in0=rising[:, 0:more], scalar1=GAMMA**done)
-            done *= 2
+        nc.vector.memset(gammas[:], GAMMA)
+        nc.vector.tensor_tensor_scan(
+            out=rising[:], data0=gammas[:], data1=gammas[:], initial=1.0, op0=ALU.mult, op1=ALU.min
+        )
         above = const.tile([P, WINDOWS], F32, name="above")
         below = const.tile([P, WINDOWS], F32, name="below")
         level = const.tile([P, WINDOWS], F32, name="level")
-        nc.vector.tensor_scalar_mul(out=above[:], in0=rising[:, ::-1], scalar1=seeds[:, 0:1])
-        nc.vector.tensor_scalar_mul(out=below[:], in0=rising[:], scalar1=seeds[:, 1:2])
-        nc.vector.tensor_tensor(out=level[:], in0=above[:], in1=below[:], op=ALU.min)
-        nc.vector.tensor_scalar_mul(out=level[:], in0=level[:], scalar1=GAMMA ** (-PASS))
+        forward = const.tile([P, WINDOWS], F32, name="forward")
+        backward = const.tile([P, WINDOWS], F32, name="backward")
+        nc.vector.tensor_scalar_mul(out=forward[:], in0=rising[:, ::-1], scalar1=seeds[:, 0:1])
+        nc.vector.tensor_scalar_mul(out=backward[:], in0=rising[:], scalar1=seeds[:, 1:2])
+        nc.vector.tensor_tensor(out=level[:], in0=forward[:], in1=backward[:], op=ALU.min)
+        for table, powers in ((above, forward), (below, backward)):
+            nc.gpsimd.tensor_scalar(
+                out=table[:], in0=powers[:], scalar1=GAMMA**PASS, scalar2=0.0, op0=ALU.mult, op1=ALU.add
+            )
         decay = {1: above, -1: below, 0: level}
 
         grouped = {}
@@ -228,7 +233,7 @@ def tile_simpleretention_pa_t_kernel(tc, q, k, x, w_v, out):
             for part in range(2):
                 bank = side_bank()
                 if b == 0 and (name, g) in FILL and part == 0:
-                    fill_clock(bank, FILL[(name, g)], BANK)
+                    fill_clock(bank, FILL[(name, g)], 2 * P)
                 for a in range(2):
                     for u in range(2):
                         first = (2 * part + a) * (H // 2) + u * P
@@ -417,9 +422,9 @@ def tile_simpleretention_pa_t_kernel(tc, q, k, x, w_v, out):
                 tensor_side(slot)
                 if slot + SCORES_AHEAD == 0:
                     pass
-                for engine in TAIL if slot >= STEPS else ("scalar", "vector", "scalar", "vector"):
+                for engine in TAIL if slot >= STEPS else PRE[slot]:
                     empty_next(engine, slot, 0)
-                if slot < 0:
+                if slot < -1:
                     vector_due(slot + 1)
                 if slot == -1:
                     for step in range(SCORES_AHEAD):

@@ -52,6 +52,7 @@ SECOND_V = (-5, 1, 6, 7)
 FIRST_LOADS = (("k", 0), ("q", 0), ("k", 1), ("q", 1), ("x", 0), ("x", 1))
 NEXT_LOADS = (("x", 0), ("k", 0), ("q", 0), ("k", 1), ("q", 1), ("x", 1))
 W_SLOT = 4
+LATE = {61: ("scalar",), 62: (), 63: ("vector",)}
 EMPTY = (("vector", "scalar"), ("scalar", "scalar"), ("vector", "scalar"), ("scalar", "scalar"), ("vector", "scalar"), ("scalar", "scalar"), ("vector", "scalar"), ("scalar", "scalar"), ("vector", "scalar"), ("scalar", "scalar"), ("vector", "scalar"), ("scalar", "scalar"), ("vector", "scalar"), ("scalar", "scalar"), ("vector", "scalar"), ("scalar", "vector"))
 FIRST_PAIRED = ROUND
 LAST_ROUND = STEPS - PACK
@@ -277,6 +278,31 @@ def tile_simpleretention_pa_t_kernel(tc, q, k, x, w_v, out):
                 )
             return [("out", (b, gq), tq, bank)]
 
+        def tensor_last_out(b, gq, tq):
+            banks = []
+            for half in range(2):
+                bank = side_bank()
+                for gk in range(2):
+                    matmul_mx(
+                        bank[:, 0 : 2 * P],
+                        codes[("g", b, gq, gk)],
+                        tq * P,
+                        codes[("v", b, gk)],
+                        half * 2 * P,
+                        2 * P,
+                        start=(gk == 0),
+                        stop=(gk == 1),
+                    )
+                banks.append(("last", (b, gq), half, bank))
+            return banks
+
+        def empty_last(engine, key, half, bank):
+            b, gq = key
+            piece = slice((PACK - 1) * BANK + half * 2 * P, (PACK - 1) * BANK + (half + 1) * 2 * P)
+            empty_bank(engine, staged[key][:, piece], bank[:, 0 : 2 * P])
+            rows = out[b].rearrange("(g j t) h -> g t j h", g=2, j=P, t=PACK)
+            nc.sync.dma_start(out=rows[gq, PACK - 1][:, half * 2 * P : (half + 1) * 2 * P], in_=staged[key][:, piece])
+
         staged = {}
 
         def empty_out(engine, key, tq, bank):
@@ -284,7 +310,7 @@ def tile_simpleretention_pa_t_kernel(tc, q, k, x, w_v, out):
                 staged[key] = work.tile([P, PACK * BANK], F32, name="staged", tag="staged", bufs=STAGED_BUFS)
             empty_bank(engine, staged[key][:, tq * BANK : (tq + 1) * BANK], bank[:])
             b, gq = key
-            if key == (B - 1, 1):
+            if b == B - 1:
                 rows = out[b].rearrange("(g j t) h -> g t j h", g=2, j=P, t=PACK)
                 nc.sync.dma_start(out=rows[gq, tq], in_=staged[key][:, tq * BANK : (tq + 1) * BANK])
             elif tq == PACK - 1:
@@ -381,6 +407,8 @@ def tile_simpleretention_pa_t_kernel(tc, q, k, x, w_v, out):
                     banks = tensor_transposes(job[1], job[2], job[3])
                 elif job[0] == "v":
                     banks = tensor_v(job[1], job[2], job[3])
+                elif job[1:] == (B - 1, 1, PACK - 1):
+                    banks = tensor_last_out(job[1], job[2], job[3])
                 else:
                     banks = tensor_out(job[1], job[2], job[3])
                 for item in banks:
@@ -403,6 +431,8 @@ def tile_simpleretention_pa_t_kernel(tc, q, k, x, w_v, out):
                 empty_v(engine, key, part, bank)
                 if part == PACK - 1:
                     later(slot + 1, quantise, key)
+            elif kind == "last":
+                empty_last(engine, key, part, bank)
             else:
                 empty_out(engine, key, part, bank)
 
@@ -441,7 +471,7 @@ def tile_simpleretention_pa_t_kernel(tc, q, k, x, w_v, out):
                     if slot >= EARLY_SWISH:
                         scalar_swish(slot, slot)
                 elif piece == "E":
-                    for engine in EMPTY[i % len(EMPTY)]:
+                    for engine in LATE.get(slot, EMPTY[i % len(EMPTY)]):
                         empty_next(engine, slot, 1)
                 elif piece == "Q":
                     vector_due(slot)

@@ -35,7 +35,7 @@ HALVED_LOADS = 2
 G_LAG = 1
 T_LAG = 1
 EARLY_SWISH = 63
-ORDER = "SDEQ"
+FREE_FROM = 6
 FILL = {("k", 0): 8, ("q", 0): 4, ("k", 1): 4}
 HEAD_SCORES = -1
 FIRST_SLOT = -3
@@ -53,7 +53,7 @@ FIRST_LOADS = (("k", 0), ("q", 0), ("k", 1), ("q", 1), ("x", 0), ("x", 1))
 NEXT_LOADS = (("x", 0), ("k", 0), ("q", 0), ("k", 1), ("q", 1), ("x", 1))
 W_SLOT = 4
 LATE = {61: ("scalar",), 62: (), 63: ("vector",)}
-EMPTY = (("vector", "scalar"), ("scalar", "scalar"), ("vector", "scalar"), ("scalar", "scalar"), ("vector", "scalar"), ("scalar", "scalar"), ("vector", "scalar"), ("scalar", "scalar"), ("vector", "scalar"), ("scalar", "scalar"), ("vector", "scalar"), ("scalar", "scalar"), ("vector", "scalar"), ("scalar", "scalar"), ("vector", "scalar"), ("scalar", "vector"))
+EMPTY = (("vector", "scalar"), ("scalar", "scalar"))
 FIRST_PAIRED = ROUND
 LAST_ROUND = STEPS - PACK
 
@@ -442,16 +442,11 @@ def tile_simpleretention_pa_t_kernel(tc, q, k, x, w_v, out):
             for item in due:
                 item[1](item[2])
 
-        ctx.enter_context(tc.manual_schedule())
-        regroup_w(("w",))
-        for slot in range(FIRST_SLOT, last_slot + 4):
-            i = slot % STEPS_PER_SEQ
+        def run_slot(slot):
             if slot < 0 or slot >= STEPS:
                 if slot >= STEPS:
                     vector_due(slot)
                 tensor_side(slot)
-                if slot + SCORES_AHEAD == 0:
-                    pass
                 for engine in TAIL if slot >= STEPS else PRE[slot]:
                     empty_next(engine, slot, 0)
                 if slot < -1:
@@ -459,19 +454,23 @@ def tile_simpleretention_pa_t_kernel(tc, q, k, x, w_v, out):
                 if slot == -1:
                     for step in range(SCORES_AHEAD):
                         tensor_scores(step)
-                continue
+                return
             if slot + SCORES_AHEAD < STEPS:
                 tensor_scores(slot + SCORES_AHEAD)
             tensor_side(slot)
-            for piece in ORDER:
-                if piece == "S" and 1 <= slot <= EARLY_SWISH:
-                    scalar_swish(slot - 1, slot)
-                elif piece == "D":
-                    vector_decay(slot)
-                    if slot >= EARLY_SWISH:
-                        scalar_swish(slot, slot)
-                elif piece == "E":
-                    for engine in LATE.get(slot, EMPTY[i % len(EMPTY)]):
-                        empty_next(engine, slot, 1)
-                elif piece == "Q":
-                    vector_due(slot)
+            if 1 <= slot <= EARLY_SWISH:
+                scalar_swish(slot - 1, slot)
+            vector_decay(slot)
+            if slot >= EARLY_SWISH:
+                scalar_swish(slot, slot)
+            for engine in LATE.get(slot, EMPTY[slot % len(EMPTY)]):
+                empty_next(engine, slot, 1)
+            vector_due(slot)
+
+        with tc.manual_schedule():
+            regroup_w(("w",))
+            for slot in range(FIRST_SLOT, FREE_FROM):
+                run_slot(slot)
+        with tc.manual_schedule(engines={mybir.EngineType.PE, mybir.EngineType.Activation, mybir.EngineType.SP}):
+            for slot in range(FREE_FROM, last_slot + 4):
+                run_slot(slot)

@@ -471,6 +471,5 @@ def tile_simpleretention_pa_t_kernel(tc, q, k, x, w_v, out):
             regroup_w(("w",))
             for slot in range(FIRST_SLOT, FREE_FROM):
                 run_slot(slot)
-        with tc.manual_schedule(engines={mybir.EngineType.PE, mybir.EngineType.Activation, mybir.EngineType.SP}):
-            for slot in range(FREE_FROM, last_slot + 4):
-                run_slot(slot)
+        for slot in range(FREE_FROM, last_slot + 4):
+            run_slot(slot)

@@ -24,8 +24,8 @@ GROUP = PASS * PACK
 ROUND = 2 * PACK
 STEPS_PER_SEQ = 2 * ROUND
 STEPS = B * STEPS_PER_SEQ
-SCORE_BANKS = 4
-SIDE_BANKS = 4
+SCORE_BANKS = 3
+SIDE_BANKS = 5
 SCORES_AHEAD = 2
 
 S_TWICE = (2, 5, 7, 10, 14)

@@ -31,12 +31,11 @@ SCORES_AHEAD = 2
 S_TWICE = (2, 5, 7, 10, 14)
 V_SIDE = (1, 4, 7, 9, 11, 13, 15)
 
-HALVED_LOADS = 2
+HALVED_LOADS = 3
 G_LAG = 1
 T_LAG = 1
 EARLY_SWISH = 63
 FREE_FROM = 6
-FILL = {("k", 0): 8, ("q", 0): 4, ("k", 1): 4}
 HEAD_SCORES = -1
 FIRST_SLOT = -3
 TILES = ((("x", 0), -12), (("k", 0), -8), (("q", 0), -6), (("k", 1), -4), (("q", 1), 0), (("x", 1), 2))
@@ -99,13 +98,6 @@ def tile_simpleretention_pa_t_kernel(tc, q, k, x, w_v, out):
                     out=w_rows[:].rearrange("p (u f) -> p u f", u=2),
                     in_=w_v.rearrange("(u p e) c -> p u (e c)", u=2, p=P, e=2),
                 )
-
-        zeros = const.tile([P, 2 * P], BF16, name="zeros")
-        nc.vector.memset(zeros[:], 0.0)
-
-        def fill_clock(bank, count, width):
-            for step in range(count):
-                nc.tensor.matmul(out=bank[:, 0:width], lhsT=zeros[:, 0:P], rhs=zeros[:, 0:width], start=True, stop=True)
 
         base = const.tile([P, 2], F32, name="base")
         exponents = const.tile([P, 2], F32, name="exponents")
@@ -233,8 +225,6 @@ def tile_simpleretention_pa_t_kernel(tc, q, k, x, w_v, out):
             banks = []
             for part in range(2):
                 bank = side_bank()
-                if b == 0 and (name, g) in FILL and part == 0:
-                    fill_clock(bank, FILL[(name, g)], 2 * P)
                 for a in range(2):
                     for u in range(2):
                         first = (2 * part + a) * (H // 2) + u * P

from contextlib import ExitStack

import concourse.mybir as mybir
from concourse.masks import make_identity

F32 = mybir.dt.float32
BF16 = mybir.dt.bfloat16
U32 = mybir.dt.uint32
U8 = mybir.dt.uint8
FP8X4 = mybir.dt.float8_e4m3fn_x4
ALU = mybir.AluOpType
ACT = mybir.ActivationFunctionType

B, S, H = 4, 1024, 512
GAMMA = 0.96875
FLOPS = 2 * B * S * H * H + 4 * B * S * S * H

P = 128
PACK = 4
PASS = P * PACK
BANK = 512
GROUP = PASS * PACK

ROUND = 2 * PACK
STEPS_PER_SEQ = 2 * ROUND
STEPS = B * STEPS_PER_SEQ
SCORE_BANKS = 3
SIDE_BANKS = 5
SCORES_AHEAD = 2

S_TWICE = (2, 5, 7, 10, 14)
V_SIDE = (1, 4, 7, 9, 11, 13, 15)

HALVED_LOADS = 3
G_LAG = 1
T_LAG = 1
EARLY_SWISH = 63
FREE_FROM = 6
HEAD_SCORES = -1
FIRST_SLOT = -3
TILES = ((("x", 0), -12), (("k", 0), -8), (("q", 0), -6), (("k", 1), -4), (("q", 1), 0), (("x", 1), 2))
V_PARTS = (-7, 1, 6, 7)
OUT_SLOTS = ((11, 14), (19, 21))
HEAD_TILES = ((("k", 0), -3), (("q", 0), -2), (("k", 1), -1), (("q", 1), 0), (("x", 0), 1), (("x", 1), 2))
HEAD_V = (5, 6, 7, 9)
PRE = {-3: ("scalar", "vector"), -2: ("scalar", "vector"), -1: ("scalar", "scalar")}
LAST_OUT = ((11, 12), (17, 18))
TAIL = ("scalar", "vector", "scalar", "vector")
HEAD_OUT = ((14, 15), (19, 21))
SECOND_V = (-5, 1, 6, 7)
FIRST_LOADS = (("k", 0), ("q", 0), ("k", 1), ("q", 1), ("x", 0), ("x", 1))
NEXT_LOADS = (("x", 0), ("k", 0), ("q", 0), ("k", 1), ("q", 1), ("x", 1))
W_SLOT = 4
LATE = {61: ("scalar",), 62: (), 63: ("vector",)}
EMPTY = (("vector", "scalar"), ("scalar", "scalar"))
FIRST_PAIRED = ROUND
LAST_ROUND = STEPS - PACK

WINDOWS = BANK + PACK - 1

LOAD_BUFS = 6
CODE_BUFS = {"k": 4, "q": 4, "x": 3, "v": 6, "g": 6, "w": 1}
GROUPED_BUFS = 6
SWISH_BUFS = 4
DECAYED_BUFS = 4
STAGED_BUFS = 3


def tile_simpleretention_pa_t_kernel(tc, q, k, x, w_v, out):
    nc = tc.nc
    inputs = {"q": q, "k": k, "x": x}
    with ExitStack() as ctx:
        const = ctx.enter_context(tc.tile_pool(name="const", bufs=1))
        loads = ctx.enter_context(tc.tile_pool(name="loads", bufs=LOAD_BUFS))
        work = ctx.enter_context(tc.tile_pool(name="work", bufs=2))
        psum = ctx.enter_context(tc.psum_pool(name="psum", bufs=1))

        loaded = {}
        place = {}

        def load(name, b, g):
            place[(name, b, g)] = len(place) + (1 if len(place) >= 7 else 0)
            tile = loads.tile([P, GROUP], BF16, name="in_" + name, tag="in_" + name, bufs=LOAD_BUFS)
            rows = inputs[name][b].rearrange("(g p t) h -> g p (t h)", g=2, p=P, t=PACK)[g]
            if len(place) <= HALVED_LOADS:
                nc.sync.dma_start(out=tile[:, 0 : GROUP // 2], in_=rows[:, 0 : GROUP // 2])
                nc.sync.dma_start(out=tile[:, GROUP // 2 : GROUP], in_=rows[:, GROUP // 2 : GROUP])
            else:
                nc.sync.dma_start(out=tile[:], in_=rows)
            loaded[(name, b, g)] = tile

        w_rows = const.tile([P, GROUP], BF16, name="w_rows")
        for b in range(B):
            for name, g in FIRST_LOADS if b == 0 else NEXT_LOADS:
                load(name, b, g)
            if b == 0:
                nc.sync.dma_start(
                    out=w_rows[:].rearrange("p (u f) -> p u f", u=2),
                    in_=w_v.rearrange("(u p e) c -> p u (e c)", u=2, p=P, e=2),
                )

        base = const.tile([P, 2], F32, name="base")
        exponents = const.tile([P, 2], F32, name="exponents")
        seeds = const.tile([P, 2], F32, name="seeds")
        nc.gpsimd.memset(base[:], GAMMA)
        nc.gpsimd.iota(
            exponents[:, 0:1], [[1, 1]], base=-PASS, channel_multiplier=PACK, allow_small_or_imprecise_dtypes=True
        )
        nc.gpsimd.iota(
            exponents[:, 1:2], [[1, 1]], base=-4, channel_multiplier=-PACK, allow_small_or_imprecise_dtypes=True
        )
        nc.gpsimd.tensor_tensor(out=seeds[:], in0=base[:], in1=exponents[:], op=ALU.pow)

        ident = const.tile([P, P], F32, name="ident")
        make_identity(nc, ident[:])

        gammas = const.tile([P, WINDOWS], F32, name="gammas")
        rising = const.tile([P, WINDOWS], F32, name="rising")
        nc.vector.memset(gammas[:], GAMMA)
        nc.vector.tensor_tensor_scan(
            out=rising[:], data0=gammas[:], data1=gammas[:], initial=1.0, op0=ALU.mult, op1=ALU.min
        )
        above = const.tile([P, WINDOWS], F32, name="above")
        below = const.tile([P, WINDOWS], F32, name="below")
        level = const.tile([P, WINDOWS], F32, name="level")
        forward = const.tile([P, WINDOWS], F32, name="forward")
        backward = const.tile([P, WINDOWS], F32, name="backward")
        nc.vector.tensor_scalar_mul(out=forward[:], in0=rising[:, ::-1], scalar1=seeds[:, 0:1])
        nc.vector.tensor_scalar_mul(out=backward[:], in0=rising[:], scalar1=seeds[:, 1:2])
        nc.vector.tensor_tensor(out=level[:], in0=forward[:], in1=backward[:], op=ALU.min)
        for table, powers in ((above, forward), (below, backward)):
            nc.gpsimd.tensor_scalar(
                out=table[:], in0=powers[:], scalar1=GAMMA**PASS, scalar2=0.0, op0=ALU.mult, op1=ALU.add
            )
        decay = {1: above, -1: below, 0: level}

        grouped = {}
        codes = {}
        quantised = set()
        out_ready = []

        def empty_bank(engine, dst, src):
            if engine == "scalar":
                nc.scalar.copy(out=dst, in_=src)
            else:
                nc.vector.tensor_copy(out=dst, in_=src)

        def new_grouped(key):
            if key[0] == "w":
                grouped[key] = const.tile([P, GROUP], BF16, name="w_grouped", align_bytes=64)
            elif key[0] == "g":
                grouped[key] = work.tile([P, GROUP], BF16, name="swish", tag="swish", bufs=SWISH_BUFS, align_bytes=64)
            else:
                grouped[key] = work.tile([P, GROUP], BF16, name="grouped", tag="grouped", bufs=GROUPED_BUFS, align_bytes=64)

        def new_codes(key):
            kind = key[0]
            words = work.tile(
                [P, PASS], U32, name="words_" + kind, tag="words_" + kind, bufs=CODE_BUFS[kind], align_bytes=64
            )
            scales = work.tile(
                [P, PASS], U8, name="scales_" + kind, tag="scales_" + kind, bufs=CODE_BUFS[kind], align_bytes=64
            )
            codes[key] = (words, scales)

        def quantise(key):
            new_codes(key)
            words, scales = codes[key]
            nc.vector.quantize_mx(out=words[:].bitcast(FP8X4), scales=scales[:], in_=grouped[key][:])
            quantised.add(key)
            if key[0] == "q":
                quantised.add((key, 0))
                quantised.add((key, 1))
            if key[0] == "g" and key[3] == 1:
                for tq in range(PACK):
                    out_ready.append((key[1], key[2], tq))

        def quantise_bank(key_and_part):
            key, part = key_and_part
            if part == 0:
                new_codes(key)
            words, scales = codes[key]
            nc.vector.quantize_mx(
                out=words[:, part * 2 * P : (part + 1) * 2 * P].bitcast(FP8X4),
                scales=scales[:, part * 2 * P : (part + 1) * 2 * P],
                in_=grouped[key][:, part * 2 * BANK : (part + 1) * 2 * BANK],
            )
            quantised.add((key, part))
            if part == 1:
                quantised.add(key)

        def quantise_query_block(key_and_block):
            key, tq = key_and_block
            if tq == 0:
                new_codes(key)
            words, scales = codes[key]
            nc.vector.quantize_mx(
                out=words[:, tq * P : (tq + 1) * P].bitcast(FP8X4),
                scales=scales[:, tq * P : (tq + 1) * P],
                in_=grouped[key][:, tq * BANK : (tq + 1) * BANK],
            )
            if key[3] == 1:
                out_ready.append((key[1], key[2], tq))

        def matmul_mx(dst, stationary, first_m, moving, first_n, width, start=True, stop=True):
            nc.tensor.matmul_mx(
                out=dst,
                lhsT=stationary[0][:, first_m : first_m + P].bitcast(FP8X4),
                lhsT_scale=stationary[1][:, first_m : first_m + P],
                rhs=moving[0][:, first_n : first_n + width].bitcast(FP8X4),
                rhs_scale=moving[1][:, first_n : first_n + width],
                start=start,
                stop=stop,
            )

        def four_row_tiles(bank, tokens, moving, first_n):
            for s in range(PACK):
                matmul_mx(bank[:, s * P : (s + 1) * P], tokens, (PACK - 1 - s) * P, moving, first_n, P)

        def side_bank():
            return psum.tile([P, BANK], F32, name="side", tag="side", bufs=SIDE_BANKS)

        def tensor_transposes(name, b, g):
            words = loaded[(name, b, g)][:].bitcast(F32)
            banks = []
            for part in range(2):
                bank = side_bank()
                for a in range(2):
                    for u in range(2):
                        first = (2 * part + a) * (H // 2) + u * P
                        nc.tensor.transpose(
                            out=bank[:, (2 * a + u) * P : (2 * a + u + 1) * P],
                            in_=words[:, first : first + P],
                            identity=ident[:],
                        )
                banks.append(("transposes", (name, b, g), part, bank))
            return banks

        def empty_transposes(engine, key, part, bank):
            if part == 0:
                new_grouped(key)
            dst = grouped[key][:].bitcast(F32)[:, part * BANK : (part + 1) * BANK]
            empty_bank(
                engine,
                dst.rearrange("p (a r u) -> p a r u", a=2, u=2),
                bank[:].rearrange("p (a u r) -> p a r u", a=2, u=2),
            )

        def tensor_v(b, g, part):
            bank = side_bank()
            four_row_tiles(bank, codes[("x", b, g)], codes[("w",)], part * P)
            return [("v", ("v", b, g), part, bank)]

        def empty_v(engine, key, part, bank):
            if part == 0:
                new_grouped(key)
            empty_bank(
                engine,
                grouped[key][:, part * BANK : (part + 1) * BANK].rearrange("p (w s) -> p w s", s=PACK),
                bank[:].rearrange("p (s w) -> p w s", s=PACK),
            )

        def tensor_out(b, gq, tq):
            bank = side_bank()
            for gk in range(2):
                matmul_mx(
                    bank[:], codes[("g", b, gq, gk)], tq * P, codes[("v", b, gk)], 0, BANK, start=(gk == 0), stop=(gk == 1)
                )
            return [("out", (b, gq), tq, bank)]

        def tensor_last_out(b, gq, tq):
            banks = []
            for half in range(2):
                bank = side_bank()
                for gk in range(2):
                    matmul_mx(
                        bank[:, 0 : 2 * P],
                        codes[("g", b, gq, gk)],
                        tq * P,
                        codes[("v", b, gk)],
                        half * 2 * P,
                        2 * P,
                        start=(gk == 0),
                        stop=(gk == 1),
                    )
                banks.append(("last", (b, gq), half, bank))
            return banks

        def empty_last(engine, key, half, bank):
            b, gq = key
            piece = slice((PACK - 1) * BANK + half * 2 * P, (PACK - 1) * BANK + (half + 1) * 2 * P)
            empty_bank(engine, staged[key][:, piece], bank[:, 0 : 2 * P])
            rows = out[b].rearrange("(g j t) h -> g t j h", g=2, j=P, t=PACK)
            nc.sync.dma_start(out=rows[gq, PACK - 1][:, half * 2 * P : (half + 1) * 2 * P], in_=staged[key][:, piece])

        staged = {}

        def empty_out(engine, key, tq, bank):
            if tq == 0:
                staged[key] = work.tile([P, PACK * BANK], F32, name="staged", tag="staged", bufs=STAGED_BUFS)
            empty_bank(engine, staged[key][:, tq * BANK : (tq + 1) * BANK], bank[:])
            b, gq = key
            if b == B - 1:
                rows = out[b].rearrange("(g j t) h -> g t j h", g=2, j=P, t=PACK)
                nc.sync.dma_start(out=rows[gq, tq], in_=staged[key][:, tq * BANK : (tq + 1) * BANK])
            elif tq == PACK - 1:
                rows = out[b].rearrange("(g j t) h -> g j (t h)", g=2, j=P, t=PACK)
                nc.sync.dma_start(out=rows[gq], in_=staged[key][:])

        def step_ids(i):
            return i // STEPS_PER_SEQ, (i % STEPS_PER_SEQ) // ROUND, (i % ROUND) // PACK, i % PACK

        score_bank = {}
        decayed = {}

        def tensor_scores(i):
            b, gq, gk, tq = step_ids(i)
            bank = psum.tile([P, BANK], F32, name="scores", tag="scores", bufs=SCORE_BANKS)
            four_row_tiles(bank, codes[("k", b, gk)], codes[("q", b, gq)], tq * P)
            score_bank[i] = bank

        def vector_decay(i):
            b, gq, gk, tq = step_ids(i)
            if i % 2 == 0:
                decayed[i // 2] = work.tile([P, 2 * BANK], F32, name="decayed", tag="decayed", bufs=DECAYED_BUFS)
            half = slice((i % 2) * BANK, (i % 2 + 1) * BANK)
            nc.vector.tensor_tensor(
                out=decayed[i // 2][:, half].rearrange("p (j s) -> p j s", s=PACK),
                in0=score_bank[i][:].rearrange("p (s j) -> p j s", s=PACK),
                in1=decay[gk - gq][:, tq : tq + BANK].rearrange("p (j s) -> p j s", s=PACK),
                op=ALU.mult,
            )

        def scalar_swish(i, slot):
            b, gq, gk, tq = step_ids(i)
            key = ("g", b, gq, gk)
            if i >= LAST_ROUND or i < FIRST_PAIRED:
                if tq == 0:
                    new_grouped(key)
                half = slice((i % 2) * BANK, (i % 2 + 1) * BANK)
                nc.scalar.activation(
                    out=grouped[key][:, tq * BANK : (tq + 1) * BANK], in_=decayed[i // 2][:, half], func=ACT.Silu
                )
                if i >= LAST_ROUND:
                    later(slot + 1, quantise_query_block, (key, tq))
                elif tq == PACK - 1:
                    later(slot + G_LAG, quantise, key)
            elif i % 2 == 1:
                if tq == 1:
                    new_grouped(key)
                nc.scalar.activation(
                    out=grouped[key][:, (tq - 1) * BANK : (tq + 1) * BANK], in_=decayed[i // 2][:], func=ACT.Silu
                )
                if tq == PACK - 1:
                    later(slot + G_LAG, quantise, key)

        def regroup_w(key):
            new_grouped(key)
            for part in range(PACK):
                nc.gpsimd.tensor_scalar(
                    out=grouped[key][:, part * BANK : (part + 1) * BANK].rearrange("p (c t) -> p c t", t=PACK),
                    in0=w_rows[:].rearrange("p (t c) -> p c t", t=PACK)[:, part * P : (part + 1) * P, :],
                    scalar1=1.0,
                    scalar2=0.0,
                    op0=ALU.mult,
                    op1=ALU.add,
                )

        calendar = {}

        def at_slot(slot, *jobs):
            calendar.setdefault(slot, []).extend(jobs)

        for b in range(B):
            first = b * STEPS_PER_SEQ
            for (name, g), offset in HEAD_TILES if b == 0 else TILES:
                at_slot(first + offset, ("transposes", name, b, g))
            for g in range(2):
                for part in range(PACK):
                    offset = (HEAD_V if b == 0 else SECOND_V if b == 1 else V_PARTS)[2 * g + part // 2]
                    at_slot(first + offset, ("v", b, g, part))
            for gq in range(2):
                for tq in range(PACK):
                    at_slot(first + (HEAD_OUT if b == 0 else LAST_OUT if b == B - 1 else OUT_SLOTS)[gq][tq // 2], ("out", b, gq, tq))
        filled = []
        todo = {"vector": []}

        def later(slot, function, argument):
            todo["vector"].append((slot, function, argument))

        later(W_SLOT, quantise, ("w",))
        last_slot = max(calendar)

        def tensor_side(slot):
            for job in calendar.get(slot, []):
                if job[0] == "transposes":
                    banks = tensor_transposes(job[1], job[2], job[3])
                elif job[0] == "v":
                    banks = tensor_v(job[1], job[2], job[3])
                elif job[1:] == (B - 1, 1, PACK - 1):
                    banks = tensor_last_out(job[1], job[2], job[3])
                else:
                    banks = tensor_out(job[1], job[2], job[3])
                for item in banks:
                    filled.append((slot, item[0], item[1], item[2], item[3]))
            assert len(filled) <= SIDE_BANKS, "side banks at slot %d: %d" % (slot, len(filled))

        def empty_next(engine, slot, lag):
            if len(filled) == 0 or filled[0][0] > slot - lag:
                return
            item = filled[0]
            filled.remove(item)
            kind, key, part, bank = item[1], item[2], item[3], item[4]
            if kind == "transposes":
                empty_transposes(engine, key, part, bank)
                if key[1] == 0:
                    later(slot + 1, quantise_bank, (key, part))
                elif part == 1:
                    later(slot + T_LAG, quantise, key)
            elif kind == "v":
                empty_v(engine, key, part, bank)
                if part == PACK - 1:
                    later(slot + 1, quantise, key)
            elif kind == "last":
                empty_last(engine, key, part, bank)
            else:
                empty_out(engine, key, part, bank)

        def vector_due(slot):
            due = [item for item in todo["vector"] if item[0] <= slot]
            todo["vector"] = [item for item in todo["vector"] if item[0] > slot]
            for item in due:
                item[1](item[2])

        def run_slot(slot):
            if slot < 0 or slot >= STEPS:
                if slot >= STEPS:
                    vector_due(slot)
                tensor_side(slot)
                for engine in TAIL if slot >= STEPS else PRE[slot]:
                    empty_next(engine, slot, 0)
                if slot < -1:
                    vector_due(slot + 1)
                if slot == -1:
                    for step in range(SCORES_AHEAD):
                        tensor_scores(step)
                return
            if slot + SCORES_AHEAD < STEPS:
                tensor_scores(slot + SCORES_AHEAD)
            tensor_side(slot)
            if 1 <= slot <= EARLY_SWISH:
                scalar_swish(slot - 1, slot)
            vector_decay(slot)
            if slot >= EARLY_SWISH:
                scalar_swish(slot, slot)
            for engine in LATE.get(slot, EMPTY[slot % len(EMPTY)]):
                empty_next(engine, slot, 1)
            vector_due(slot)

        with tc.manual_schedule():
            regroup_w(("w",))
            for slot in range(FIRST_SLOT, FREE_FROM):
                run_slot(slot)
        for slot in range(FREE_FROM, last_slot + 4):
            run_slot(slot)
